import numpy as np
import ml_dtypes


def mxq(x, axis, fmt="e4m3"):
    dtype, down = {"e4m3": (ml_dtypes.float8_e4m3fn, 7), "e5m2": (ml_dtypes.float8_e5m2, 14)}[fmt]
    v = np.moveaxis(np.asarray(x, np.float32).astype(ml_dtypes.bfloat16).astype(np.float64), axis, -1)
    blocks = v.reshape(v.shape[:-1] + (-1, 32))
    amax = np.abs(blocks).max(-1, keepdims=True)
    byte = np.maximum(np.where(amax > 0, np.frexp(amax)[1] - 1 + 127, 0) - down, 1)
    scale = np.exp2(byte - 127.0)
    codes = (blocks / scale).astype(np.float32).astype(dtype).astype(np.float64)
    return np.moveaxis((codes * scale).reshape(v.shape), -1, axis)


WIDE = False


def mx_kscale(k):
    if not WIDE:
        return np.ones(k)
    levels = np.array([20, -20, 10, -10, 0])
    a = np.random.permutation(np.resize(levels, k // 512 * 4)).reshape(k // 512, 4)
    idx = np.arange(k)
    return np.exp2(a[idx // 512, idx % 128 // 32])


BF16 = ml_dtypes.bfloat16


def bf(x):
    return np.asarray(x, np.float32).astype(BF16)


def f64(x):
    return np.asarray(x).astype(np.float64)


B, N, IN, H, D = 2, 64, 512, 8, 64
T = B * N * N
LN_EPS = 1e-5


def masked_edges(emb_edge, node_mask):
    m = f64(node_mask)
    return f64(emb_edge) * (m[:, :, None] * m[:, None, :])[..., None]


def pre_norm(new_node, emb_edge, node_mask, Wedge, bedge):
    xe = masked_edges(emb_edge, node_mask)
    nn = f64(new_node)
    w = f64(Wedge)
    return xe + (nn @ w[:IN])[:, :, None] + (nn @ w[IN:IN + IN])[:, None] + xe @ w[IN + IN:] + f64(bedge)


def norm_stats(y):
    mu = y.mean(-1)
    v = ((y - mu[..., None]) ** 2).mean(-1)
    return mu, 1.0 / np.sqrt(v + LN_EPS)


def setup_inputs():
    sv = mx_kscale(T)
    a = np.where(np.arange(B) % 2 == 0, sv.max(), sv.min())
    keep = np.random.random((B, N)) < 0.9
    nn0 = bf(np.random.standard_normal((B, N, IN)))
    ee0 = bf(np.random.standard_normal((B, N, N, IN)))
    node_mask = bf(keep * (0.5 + 0.5 * np.random.random((B, N))))
    Wedge = bf(np.random.standard_normal((3 * IN, IN)) / np.sqrt(IN))
    bedge = bf(np.random.standard_normal(IN) * 0.3)
    gamma_e = bf(1.0 + 0.1 * np.random.standard_normal(IN))
    beta_e = bf(0.1 * np.random.standard_normal(IN))
    g = bf(np.random.standard_normal((B, N, N, IN)) * np.exp2(np.random.randint(-12, 1, (B, N, N, 1)))
           / a[:, None, None, None])
    y = pre_norm(nn0, ee0, node_mask, Wedge, bedge)
    mu, rstd = norm_stats(y)
    return {"new_node": bf(f64(nn0) * a[:, None, None]),
            "emb_edge": bf(f64(ee0) * a[:, None, None, None]),
            "node_mask": node_mask,
            "Wedge": Wedge,
            "bedge": bedge,
            "gamma_e": gamma_e,
            "beta_e": beta_e,
            "y": np.asarray(y, np.float32),
            "mu": np.asarray(mu, np.float32),
            "rstd": np.asarray(rstd, np.float32),
            "grad_out": g}


def reference(new_node, emb_edge, node_mask, Wedge, bedge, gamma_e, beta_e, y, mu, rstd, grad_out):
    xe = masked_edges(emb_edge, node_mask)
    r = f64(rstd)[..., None]
    xhat = (f64(y) - f64(mu)[..., None]) * r
    gg = f64(grad_out) * f64(gamma_e)
    dy = r * (gg - gg.mean(-1, keepdims=True) - xhat * (gg * xhat).mean(-1, keepdims=True))
    nn = f64(new_node).reshape(B * N, IN)
    g_row = nn.T @ dy.sum(2).reshape(B * N, IN)
    g_col = nn.T @ dy.sum(1).reshape(B * N, IN)
    g_edge = mxq(xe.reshape(T, IN), 0, "e4m3").T @ mxq(dy.reshape(T, IN), 0, "e5m2")
    return np.concatenate([g_row, g_col, g_edge], 0)

@@ -1,0 +1,293 @@
+from contextlib import ExitStack
+
+import concourse.mybir as mybir
+from concourse.masks import make_identity
+
+F32 = mybir.dt.float32
+BF16 = mybir.dt.bfloat16
+U32 = mybir.dt.uint32
+U8 = mybir.dt.uint8
+E4M3_X4 = mybir.dt.float8_e4m3fn_x4
+E5M2_X4 = mybir.dt.float8_e5m2_x4
+ALU = mybir.AluOpType
+ACT = mybir.ActivationFunctionType
+AX = mybir.AxisListType
+
+P = 128
+PACK = 4
+GRAPHS = 2
+NODES = 64
+FEAT = 512
+TOKENS = GRAPHS * NODES * NODES
+K_PASS = P * PACK
+PASSES = TOKENS // K_PASS
+PASSES_PER_GRAPH = PASSES // GRAPHS
+ROWS_PER_PASS = K_PASS // NODES
+PARTS_PER_ROW = P // ROWS_PER_PASS
+FBLOCKS = FEAT // P
+ROUND = 4
+
+FLOPS = 2 * TOKENS * FEAT * FEAT + 2 * 2 * GRAPHS * NODES * FEAT * FEAT
+
+
+def tile_densegatlayer_pb_v_kernel(
+    tc, new_node, emb_edge, node_mask, Wedge, bedge, gamma_e, beta_e, y, mu, rstd, grad_out, out
+):
+    nc = tc.nc
+    emb_rows = emb_edge.rearrange("b i j f -> (b i j) f")
+    grad_rows = grad_out.rearrange("b i j f -> (b i j) f")
+    y_rows = y.rearrange("b i j f -> (b i j) f")
+
+    with ExitStack() as ctx:
+        const = ctx.enter_context(tc.tile_pool(name="const", bufs=1))
+        loads = ctx.enter_context(tc.tile_pool(name="loads", bufs=3))
+        work = ctx.enter_context(tc.tile_pool(name="work", bufs=3))
+        small = ctx.enter_context(tc.tile_pool(name="small", bufs=4))
+        codes = ctx.enter_context(tc.tile_pool(name="codes", bufs=2))
+        psum_cs = ctx.enter_context(tc.psum_pool(name="psum_cs", bufs=1))
+        psum_rs = ctx.enter_context(tc.psum_pool(name="psum_rs", bufs=2))
+        psum_mx = ctx.enter_context(tc.psum_pool(name="psum_mx", bufs=2))
+
+        ident = const.tile([P, P], F32, name="ident")
+        make_identity(nc, ident[:])
+
+        mask_all = const.tile([P, P], BF16, name="mask_all")
+        nc.scalar.dma_start(out=mask_all[:], in_=node_mask.rearrange("b n -> (b n)").partition_broadcast(P))
+        gamma_bc = const.tile([P, FEAT], BF16, name="gamma_bc")
+        nc.scalar.dma_start(out=gamma_bc[:], in_=gamma_e.partition_broadcast(P))
+        rstd_t = const.tile([P, PASSES, PACK], F32, name="rstd_t")
+        nc.scalar.dma_start(
+            out=rstd_t[:], in_=rstd.rearrange("b i j -> (b i j)").rearrange("(c p s) -> p c s", p=P, s=PACK)
+        )
+        mu_t = const.tile([P, PASSES, PACK], F32, name="mu_t")
+        nc.scalar.dma_start(
+            out=mu_t[:], in_=mu.rearrange("b i j -> (b i j)").rearrange("(c p s) -> p c s", p=P, s=PACK)
+        )
+        node_bf = const.tile([P, FEAT], BF16, name="node_bf")
+        nc.scalar.dma_start(out=node_bf[:], in_=new_node.rearrange("b n f -> (b n) f"))
+        node_f32 = const.tile([P, FEAT], F32, name="node_f32")
+        nc.vector.tensor_copy(out=node_f32[:], in_=node_bf[:])
+
+        sel_row = const.tile([P, ROWS_PER_PASS], F32, name="sel_row")
+        nc.vector.tensor_reduce(
+            out=sel_row[:], in_=ident[:].rearrange("p (g q) -> p g q", q=PARTS_PER_ROW), axis=AX.X, op=ALU.add
+        )
+        sel_col = const.tile([P, PARTS_PER_ROW], F32, name="sel_col")
+        nc.vector.tensor_reduce(
+            out=sel_col[:], in_=ident[:].rearrange("p (g q) -> p q g", q=PARTS_PER_ROW), axis=AX.X, op=ALU.add
+        )
+        pick_i = const.tile([P, PASSES, ROWS_PER_PASS], F32, name="pick_i")
+        nc.vector.tensor_tensor(
+            out=pick_i[:],
+            in0=mask_all[:].rearrange("p (c g) -> p c g", g=ROWS_PER_PASS),
+            in1=sel_row[:].unsqueeze(1).to_broadcast([P, PASSES, ROWS_PER_PASS]),
+            op=ALU.mult,
+        )
+        mask_i = const.tile([P, PASSES], F32, name="mask_i")
+        nc.vector.tensor_reduce(out=mask_i[:], in_=pick_i[:], axis=AX.X, op=ALU.add)
+        pick_j = const.tile([P, GRAPHS * PACK, PARTS_PER_ROW], F32, name="pick_j")
+        for b in range(GRAPHS):
+            nc.vector.tensor_tensor(
+                out=pick_j[:, b * PACK : (b + 1) * PACK, :],
+                in0=mask_all[:, b * NODES : (b + 1) * NODES].rearrange("p (q s) -> p s q", s=PACK),
+                in1=sel_col[:].unsqueeze(1).to_broadcast([P, PACK, PARTS_PER_ROW]),
+                op=ALU.mult,
+            )
+        mask_j = const.tile([P, GRAPHS * PACK], F32, name="mask_j")
+        nc.vector.tensor_reduce(out=mask_j[:], in_=pick_j[:], axis=AX.X, op=ALU.add)
+        edge_mask = const.tile([P, PASSES, PACK], F32, name="edge_mask")
+        for b in range(GRAPHS):
+            graph_passes = slice(b * PASSES_PER_GRAPH, (b + 1) * PASSES_PER_GRAPH)
+            nc.vector.tensor_tensor(
+                out=edge_mask[:, graph_passes, :],
+                in0=mask_i[:, graph_passes].unsqueeze(2).to_broadcast([P, PASSES_PER_GRAPH, PACK]),
+                in1=mask_j[:, b * PACK : (b + 1) * PACK].unsqueeze(1).to_broadcast([P, PASSES_PER_GRAPH, PACK]),
+                op=ALU.mult,
+            )
+        neg_r2 = const.tile([P, PASSES, PACK], F32, name="neg_r2")
+        nc.vector.scalar_tensor_tensor(
+            out=neg_r2[:].rearrange("p c s -> p (c s)"),
+            in0=rstd_t[:].rearrange("p c s -> p (c s)"),
+            scalar=-1.0 / FEAT,
+            in1=rstd_t[:].rearrange("p c s -> p (c s)"),
+            op0=ALU.mult,
+            op1=ALU.mult,
+        )
+
+        row_sums_t = const.tile([P, FBLOCKS, P], F32, name="row_sums_t")
+        col_sums_t = const.tile([P, FBLOCKS, P], F32, name="col_sums_t")
+        edge_acc = const.tile([P, FBLOCKS, FEAT], F32, name="edge_acc")
+
+        state = {}
+
+        def load(c):
+            rows = slice(c * K_PASS, (c + 1) * K_PASS)
+            g_raw = loads.tile([P, PACK, FEAT], BF16, name="g_raw")
+            nc.sync.dma_start(out=g_raw[:], in_=grad_rows[rows, :].rearrange("(p s) f -> p s f", s=PACK))
+            y_raw = loads.tile([P, PACK, FEAT], F32, name="y_raw", bufs=4)
+            nc.sync.dma_start(out=y_raw[:], in_=y_rows[rows, :].rearrange("(p s) f -> p s f", s=PACK))
+            e_raw = loads.tile([P, PACK, FEAT], BF16, name="e_raw")
+            nc.sync.dma_start(out=e_raw[:], in_=emb_rows[rows, :].rearrange("(p s) f -> p s f", s=PACK))
+            state[("g", c)] = g_raw
+            state[("y", c)] = y_raw
+            state[("e", c)] = e_raw
+
+        def regroup(dst, src):
+            nc.scalar.copy(
+                out=dst[:].rearrange("p (c i) s -> p c s i", i=4),
+                in_=src[:].rearrange("p s (c i) -> p c s i", i=4),
+            )
+
+        def statistics(c):
+            g_raw, y_raw, e_raw = state[("g", c)], state[("y", c)], state[("e", c)]
+            grr = work.tile([P, PACK, FEAT], F32, name="grr")
+            junk = work.tile([P, PACK, FEAT], BF16, name="junk", bufs=2)
+            sum_g = small.tile([P, PACK], F32, name="sum_g")
+            sum_gy = small.tile([P, PACK], F32, name="sum_gy")
+            for s in range(PACK):
+                nc.vector.scalar_tensor_tensor(
+                    out=grr[:, s, :], in0=g_raw[:, s, :], scalar=rstd_t[:, c, s : s + 1], in1=gamma_bc[:],
+                    op0=ALU.mult, op1=ALU.mult, accum_out=sum_g[:, s : s + 1],
+                )
+            for s in range(PACK):
+                nc.vector.scalar_tensor_tensor(
+                    out=junk[:, s, :], in0=y_raw[:, s, :], scalar=mu_t[:, c, s : s + 1], in1=grr[:, s, :],
+                    op0=ALU.subtract, op1=ALU.mult, accum_out=sum_gy[:, s : s + 1],
+                )
+            slope = small.tile([P, PACK], F32, name="slope")
+            nc.vector.tensor_tensor(out=slope[:], in0=neg_r2[:, c, :], in1=sum_gy[:], op=ALU.mult)
+            slope_mu = small.tile([P, PACK], F32, name="slope_mu")
+            nc.vector.tensor_tensor(out=slope_mu[:], in0=slope[:], in1=mu_t[:, c, :], op=ALU.mult)
+            shift = small.tile([P, PACK], F32, name="shift")
+            nc.vector.scalar_tensor_tensor(
+                out=shift[:], in0=sum_g[:], scalar=-1.0 / FEAT, in1=slope_mu[:], op0=ALU.mult, op1=ALU.subtract
+            )
+            state[("grr", c)] = grr
+            state[("slope", c)] = slope
+            state[("shift", c)] = shift
+            xe_lin = work.tile([P, PACK, FEAT], BF16, name="xe_lin", bufs=2)
+            for s in range(PACK):
+                nc.scalar.activation(
+                    out=xe_lin[:, s, :], in_=e_raw[:, s, :], func=ACT.Copy, scale=edge_mask[:, c, s : s + 1]
+                )
+            xe_grp = work.tile([P, FEAT, PACK], BF16, name="xe_grp", align_bytes=64)
+            regroup(xe_grp, xe_lin)
+            state[("xe_grp", c)] = xe_grp
+
+        def apply(c):
+            y_raw, grr = state[("y", c)], state[("grr", c)]
+            slope, shift = state[("slope", c)], state[("shift", c)]
+            for s in range(PACK):
+                nc.scalar.activation(
+                    out=y_raw[:, s, :], in_=y_raw[:, s, :], func=ACT.Identity,
+                    scale=slope[:, s : s + 1], bias=shift[:, s : s + 1],
+                )
+            nc.vector.tensor_tensor(
+                out=grr[:].rearrange("p s f -> p (s f)"),
+                in0=grr[:].rearrange("p s f -> p (s f)"),
+                in1=y_raw[:].rearrange("p s f -> p (s f)"),
+                op=ALU.add,
+            )
+            dy = grr
+            dy_grp = work.tile([P, FEAT, PACK], BF16, name="dy_grp", align_bytes=64)
+            regroup(dy_grp, dy)
+            state[("dy_grp", c)] = dy_grp
+            first_of_graph = c % PASSES_PER_GRAPH == 0
+            last_of_graph = c % PASSES_PER_GRAPH == PASSES_PER_GRAPH - 1
+            if first_of_graph:
+                for s in range(PACK):
+                    state[("cs", c // PASSES_PER_GRAPH, s)] = psum_cs.tile([P, FEAT], F32, name="cs%d" % s)
+            rs_ps = psum_rs.tile([P, FEAT], F32, name="rs_ps")
+            for s in range(PACK):
+                for k in range(FBLOCKS):
+                    nc.tensor.matmul(
+                        out=rs_ps[:, k * P : (k + 1) * P], lhsT=dy[:, s, k * P : (k + 1) * P], rhs=ident[:],
+                        is_transpose=True,
+                        start=(s == 0 and k == 0), stop=(s == PACK - 1 and k == FBLOCKS - 1),
+                    )
+            for s in range(PACK):
+                cs_ps = state[("cs", c // PASSES_PER_GRAPH, s)]
+                for k in range(FBLOCKS):
+                    nc.tensor.matmul(
+                        out=cs_ps[:, k * P : (k + 1) * P], lhsT=dy[:, s, k * P : (k + 1) * P], rhs=ident[:],
+                        is_transpose=True,
+                        start=(first_of_graph and k == 0), stop=(last_of_graph and k == FBLOCKS - 1),
+                    )
+            state[("rs", c)] = rs_ps
+
+        def finish(c):
+            g = c % ROUND
+            if g == 0:
+                state["x_codes"] = codes.tile([P, ROUND, FEAT], U32, name="x_codes", align_bytes=64)
+                state["x_scales"] = codes.tile([P, ROUND, FEAT], U8, name="x_scales", align_bytes=64)
+                state["d_codes"] = codes.tile([P, ROUND, FEAT], U32, name="d_codes", align_bytes=64)
+                state["d_scales"] = codes.tile([P, ROUND, FEAT], U8, name="d_scales", align_bytes=64)
+            x_codes, x_scales = state["x_codes"], state["x_scales"]
+            d_codes, d_scales = state["d_codes"], state["d_scales"]
+            nc.vector.quantize_mx(
+                out=x_codes[:, g, :].bitcast(E4M3_X4), scales=x_scales[:, g, :],
+                in_=state[("xe_grp", c)][:].rearrange("p f s -> p (f s)"),
+            )
+            nc.vector.quantize_mx(
+                out=d_codes[:, g, :].bitcast(E5M2_X4), scales=d_scales[:, g, :],
+                in_=state[("dy_grp", c)][:].rearrange("p f s -> p (f s)"),
+            )
+            nc.vector.tensor_reduce(
+                out=row_sums_t[:, :, c * ROWS_PER_PASS : (c + 1) * ROWS_PER_PASS],
+                in_=state[("rs", c)][:].rearrange("p (k i q) -> p k i q", k=FBLOCKS, q=PARTS_PER_ROW),
+                axis=AX.X, op=ALU.add,
+            )
+            if c % PASSES_PER_GRAPH == PASSES_PER_GRAPH - 1:
+                b = c // PASSES_PER_GRAPH
+                graph_cols = col_sums_t[:, :, b * NODES : (b + 1) * NODES].rearrange("p k (q s) -> p k q s", s=PACK)
+                for s in range(PACK):
+                    nc.vector.tensor_reduce(
+                        out=graph_cols[:, :, :, s],
+                        in_=state[("cs", b, s)][:].rearrange("p (k i q) -> p k q i", k=FBLOCKS, q=PARTS_PER_ROW),
+                        axis=AX.X, op=ALU.add,
+                    )
+            if g == ROUND - 1:
+                for m in range(FBLOCKS):
+                    m_cols = slice(m * P, (m + 1) * P)
+                    mx_ps = psum_mx.tile([P, FEAT], F32, name="mx_ps")
+                    for h in range(ROUND):
+                        nc.tensor.matmul_mx(
+                            out=mx_ps[:],
+                            lhsT=x_codes[:, h, m_cols].bitcast(E4M3_X4), lhsT_scale=x_scales[:, h, m_cols],
+                            rhs=d_codes[:, h, :].bitcast(E5M2_X4), rhs_scale=d_scales[:, h, :],
+                            start=(h == 0), stop=(h == ROUND - 1),
+                        )
+                    if c < ROUND:
+                        nc.scalar.copy(out=edge_acc[:, m, :], in_=mx_ps[:])
+                    else:
+                        nc.vector.tensor_tensor(out=edge_acc[:, m, :], in0=mx_ps[:], in1=edge_acc[:, m, :], op=ALU.add)
+                    if c == PASSES - 1:
+                        nc.sync.dma_start(out=out[2 * FEAT + m * P : 2 * FEAT + (m + 1) * P, :], in_=edge_acc[:, m, :])
+
+        load(0)
+        load(1)
+        for step in range(PASSES + 2):
+            if step + 2 < PASSES:
+                load(step + 2)
+            if step < PASSES:
+                statistics(step)
+            if 1 <= step <= PASSES:
+                apply(step - 1)
+            if step >= 2:
+                finish(step - 2)
+
+        for which, sums_t in enumerate((row_sums_t, col_sums_t)):
+            back_ps = psum_rs.tile([P, FEAT], F32, name="rs_ps")
+            for k in range(FBLOCKS):
+                nc.tensor.transpose(back_ps[:, k * P : (k + 1) * P], sums_t[:, k, :], ident[:])
+            sums = const.tile([P, FEAT], F32, name="sums%d" % which)
+            nc.scalar.copy(out=sums[:], in_=back_ps[:])
+            for m in range(FBLOCKS):
+                prod_ps = psum_cs.tile([P, FEAT], F32, name="cs%d" % m)
+                nc.tensor.matmul(out=prod_ps[:], lhsT=node_f32[:, m * P : (m + 1) * P], rhs=sums[:], start=True, stop=True)
+                prod = work.tile([P, FEAT], F32, name="prod")
+                if m % 2 == 0:
+                    nc.scalar.copy(out=prod[:], in_=prod_ps[:])
+                else:
+                    nc.vector.tensor_copy(out=prod[:], in_=prod_ps[:])
+                nc.sync.dma_start(out=out[which * FEAT + m * P : which * FEAT + (m + 1) * P, :], in_=prod[:])

@@ -26,6 +26,7 @@ ROWS_PER_PASS = K_PASS // NODES
 PARTS_PER_ROW = P // ROWS_PER_PASS
 FBLOCKS = FEAT // P
 ROUND = 4
+LAG = 3
 
 FLOPS = 2 * TOKENS * FEAT * FEAT + 2 * 2 * GRAPHS * NODES * FEAT * FEAT
 
@@ -48,11 +49,25 @@ def tile_densegatlayer_pb_v_kernel(
         psum_rs = ctx.enter_context(tc.psum_pool(name="psum_rs", bufs=2))
         psum_mx = ctx.enter_context(tc.psum_pool(name="psum_mx", bufs=2))
 
-        ident = const.tile([P, P], F32, name="ident")
-        make_identity(nc, ident[:])
+        state = {}
 
-        mask_all = const.tile([P, P], BF16, name="mask_all")
-        nc.scalar.dma_start(out=mask_all[:], in_=node_mask.rearrange("b n -> (b n)").partition_broadcast(P))
+        def pass_rows(rows_of, c):
+            return rows_of[c * K_PASS : (c + 1) * K_PASS, :].rearrange("(p s) f -> p s f", s=PACK)
+
+        def load_gradient(c):
+            g_raw = loads.tile([P, PACK, FEAT], BF16, name="g_raw")
+            nc.sync.dma_start(out=g_raw[:], in_=pass_rows(grad_rows, c))
+            y_raw = loads.tile([P, PACK, FEAT], F32, name="y_raw", bufs=4)
+            nc.sync.dma_start(out=y_raw[:], in_=pass_rows(y_rows, c))
+            state[("g", c)] = g_raw
+            state[("y", c)] = y_raw
+
+        def load_edges(c):
+            e_raw = loads.tile([P, PACK, FEAT], BF16, name="e_raw")
+            nc.sync.dma_start(out=e_raw[:], in_=pass_rows(emb_rows, c))
+            state[("e", c)] = e_raw
+
+        load_gradient(0)
         gamma_bc = const.tile([P, FEAT], BF16, name="gamma_bc")
         nc.scalar.dma_start(out=gamma_bc[:], in_=gamma_e.partition_broadcast(P))
         rstd_t = const.tile([P, PASSES, PACK], F32, name="rstd_t")
@@ -63,74 +78,63 @@ def tile_densegatlayer_pb_v_kernel(
         nc.scalar.dma_start(
             out=mu_t[:], in_=mu.rearrange("b i j -> (b i j)").rearrange("(c p s) -> p c s", p=P, s=PACK)
         )
+        load_gradient(1)
+        mask_all = const.tile([P, P], BF16, name="mask_all")
+        nc.scalar.dma_start(out=mask_all[:], in_=node_mask.rearrange("b n -> (b n)").partition_broadcast(P))
         node_bf = const.tile([P, FEAT], BF16, name="node_bf")
         nc.scalar.dma_start(out=node_bf[:], in_=new_node.rearrange("b n f -> (b n) f"))
-        node_f32 = const.tile([P, FEAT], F32, name="node_f32")
-        nc.vector.tensor_copy(out=node_f32[:], in_=node_bf[:])
+        ident = const.tile([P, P], F32, name="ident")
+        make_identity(nc, ident[:])
 
-        sel_row = const.tile([P, ROWS_PER_PASS], F32, name="sel_row")
-        nc.vector.tensor_reduce(
-            out=sel_row[:], in_=ident[:].rearrange("p (g q) -> p g q", q=PARTS_PER_ROW), axis=AX.X, op=ALU.add
-        )
-        sel_col = const.tile([P, PARTS_PER_ROW], F32, name="sel_col")
-        nc.vector.tensor_reduce(
-            out=sel_col[:], in_=ident[:].rearrange("p (g q) -> p q g", q=PARTS_PER_ROW), axis=AX.X, op=ALU.add
-        )
-        pick_i = const.tile([P, PASSES, ROWS_PER_PASS], F32, name="pick_i")
-        nc.vector.tensor_tensor(
-            out=pick_i[:],
-            in0=mask_all[:].rearrange("p (c g) -> p c g", g=ROWS_PER_PASS),
-            in1=sel_row[:].unsqueeze(1).to_broadcast([P, PASSES, ROWS_PER_PASS]),
-            op=ALU.mult,
-        )
-        mask_i = const.tile([P, PASSES], F32, name="mask_i")
-        nc.vector.tensor_reduce(out=mask_i[:], in_=pick_i[:], axis=AX.X, op=ALU.add)
-        pick_j = const.tile([P, GRAPHS * PACK, PARTS_PER_ROW], F32, name="pick_j")
-        for b in range(GRAPHS):
-            nc.vector.tensor_tensor(
-                out=pick_j[:, b * PACK : (b + 1) * PACK, :],
-                in0=mask_all[:, b * NODES : (b + 1) * NODES].rearrange("p (q s) -> p s q", s=PACK),
-                in1=sel_col[:].unsqueeze(1).to_broadcast([P, PACK, PARTS_PER_ROW]),
-                op=ALU.mult,
-            )
-        mask_j = const.tile([P, GRAPHS * PACK], F32, name="mask_j")
-        nc.vector.tensor_reduce(out=mask_j[:], in_=pick_j[:], axis=AX.X, op=ALU.add)
-        edge_mask = const.tile([P, PASSES, PACK], F32, name="edge_mask")
-        for b in range(GRAPHS):
-            graph_passes = slice(b * PASSES_PER_GRAPH, (b + 1) * PASSES_PER_GRAPH)
-            nc.vector.tensor_tensor(
-                out=edge_mask[:, graph_passes, :],
-                in0=mask_i[:, graph_passes].unsqueeze(2).to_broadcast([P, PASSES_PER_GRAPH, PACK]),
-                in1=mask_j[:, b * PACK : (b + 1) * PACK].unsqueeze(1).to_broadcast([P, PASSES_PER_GRAPH, PACK]),
-                op=ALU.mult,
-            )
-        neg_r2 = const.tile([P, PASSES, PACK], F32, name="neg_r2")
+        coef = const.tile([P, PASSES, 2, PACK], F32, name="coef")
         nc.vector.scalar_tensor_tensor(
-            out=neg_r2[:].rearrange("p c s -> p (c s)"),
-            in0=rstd_t[:].rearrange("p c s -> p (c s)"),
-            scalar=-1.0 / FEAT,
-            in1=rstd_t[:].rearrange("p c s -> p (c s)"),
-            op0=ALU.mult,
-            op1=ALU.mult,
+            out=coef[:, :, 0, :], in0=rstd_t[:], scalar=-1.0 / FEAT, in1=rstd_t[:], op0=ALU.mult, op1=ALU.mult
         )
+        nc.vector.tensor_tensor(out=coef[:, :, 1, :], in0=coef[:, :, 0, :], in1=mu_t[:], op=ALU.mult)
 
         row_sums_t = const.tile([P, FBLOCKS, P], F32, name="row_sums_t")
         col_sums_t = const.tile([P, FBLOCKS, P], F32, name="col_sums_t")
         edge_acc = const.tile([P, FBLOCKS, FEAT], F32, name="edge_acc")
+        edge_mask = const.tile([P, PASSES, PACK], F32, name="edge_mask")
+        node_f32 = const.tile([P, FEAT], F32, name="node_f32")
 
-        state = {}
-
-        def load(c):
-            rows = slice(c * K_PASS, (c + 1) * K_PASS)
-            g_raw = loads.tile([P, PACK, FEAT], BF16, name="g_raw")
-            nc.sync.dma_start(out=g_raw[:], in_=grad_rows[rows, :].rearrange("(p s) f -> p s f", s=PACK))
-            y_raw = loads.tile([P, PACK, FEAT], F32, name="y_raw", bufs=4)
-            nc.sync.dma_start(out=y_raw[:], in_=y_rows[rows, :].rearrange("(p s) f -> p s f", s=PACK))
-            e_raw = loads.tile([P, PACK, FEAT], BF16, name="e_raw")
-            nc.sync.dma_start(out=e_raw[:], in_=emb_rows[rows, :].rearrange("(p s) f -> p s f", s=PACK))
-            state[("g", c)] = g_raw
-            state[("y", c)] = y_raw
-            state[("e", c)] = e_raw
+        def build_edge_mask():
+            nc.scalar.copy(out=node_f32[:], in_=node_bf[:])
+            sel_row = const.tile([P, ROWS_PER_PASS], F32, name="sel_row")
+            nc.vector.tensor_reduce(
+                out=sel_row[:], in_=ident[:].rearrange("p (g q) -> p g q", q=PARTS_PER_ROW), axis=AX.X, op=ALU.add
+            )
+            sel_col = const.tile([P, PARTS_PER_ROW], F32, name="sel_col")
+            nc.vector.tensor_reduce(
+                out=sel_col[:], in_=ident[:].rearrange("p (g q) -> p q g", q=PARTS_PER_ROW), axis=AX.X, op=ALU.add
+            )
+            pick_i = const.tile([P, PASSES, ROWS_PER_PASS], F32, name="pick_i")
+            nc.vector.tensor_tensor(
+                out=pick_i[:],
+                in0=mask_all[:].rearrange("p (c g) -> p c g", g=ROWS_PER_PASS),
+                in1=sel_row[:].unsqueeze(1).to_broadcast([P, PASSES, ROWS_PER_PASS]),
+                op=ALU.mult,
+            )
+            mask_i = const.tile([P, PASSES], F32, name="mask_i")
+            nc.vector.tensor_reduce(out=mask_i[:], in_=pick_i[:], axis=AX.X, op=ALU.add)
+            pick_j = const.tile([P, GRAPHS * PACK, PARTS_PER_ROW], F32, name="pick_j")
+            for b in range(GRAPHS):
+                nc.vector.tensor_tensor(
+                    out=pick_j[:, b * PACK : (b + 1) * PACK, :],
+                    in0=mask_all[:, b * NODES : (b + 1) * NODES].rearrange("p (q s) -> p s q", s=PACK),
+                    in1=sel_col[:].unsqueeze(1).to_broadcast([P, PACK, PARTS_PER_ROW]),
+                    op=ALU.mult,
+                )
+            mask_j = const.tile([P, GRAPHS * PACK], F32, name="mask_j")
+            nc.vector.tensor_reduce(out=mask_j[:], in_=pick_j[:], axis=AX.X, op=ALU.add)
+            for b in range(GRAPHS):
+                graph_passes = slice(b * PASSES_PER_GRAPH, (b + 1) * PASSES_PER_GRAPH)
+                nc.vector.tensor_tensor(
+                    out=edge_mask[:, graph_passes, :],
+                    in0=mask_i[:, graph_passes].unsqueeze(2).to_broadcast([P, PASSES_PER_GRAPH, PACK]),
+                    in1=mask_j[:, b * PACK : (b + 1) * PACK].unsqueeze(1).to_broadcast([P, PASSES_PER_GRAPH, PACK]),
+                    op=ALU.mult,
+                )
 
         def regroup(dst, src):
             nc.scalar.copy(
@@ -139,7 +143,7 @@ def tile_densegatlayer_pb_v_kernel(
             )
 
         def statistics(c):
-            g_raw, y_raw, e_raw = state[("g", c)], state[("y", c)], state[("e", c)]
+            g_raw, y_raw = state[("g", c)], state[("y", c)]
             grr = work.tile([P, PACK, FEAT], F32, name="grr")
             junk = work.tile([P, PACK, FEAT], BF16, name="junk", bufs=2)
             sum_g = small.tile([P, PACK], F32, name="sum_g")
@@ -154,33 +158,25 @@ def tile_densegatlayer_pb_v_kernel(
                     out=junk[:, s, :], in0=y_raw[:, s, :], scalar=mu_t[:, c, s : s + 1], in1=grr[:, s, :],
                     op0=ALU.subtract, op1=ALU.mult, accum_out=sum_gy[:, s : s + 1],
                 )
-            slope = small.tile([P, PACK], F32, name="slope")
-            nc.vector.tensor_tensor(out=slope[:], in0=neg_r2[:, c, :], in1=sum_gy[:], op=ALU.mult)
-            slope_mu = small.tile([P, PACK], F32, name="slope_mu")
-            nc.vector.tensor_tensor(out=slope_mu[:], in0=slope[:], in1=mu_t[:, c, :], op=ALU.mult)
+            line = small.tile([P, 2, PACK], F32, name="line")
+            nc.vector.tensor_tensor(
+                out=line[:], in0=coef[:, c, :, :], in1=sum_gy[:].unsqueeze(1).to_broadcast([P, 2, PACK]), op=ALU.mult
+            )
             shift = small.tile([P, PACK], F32, name="shift")
             nc.vector.scalar_tensor_tensor(
-                out=shift[:], in0=sum_g[:], scalar=-1.0 / FEAT, in1=slope_mu[:], op0=ALU.mult, op1=ALU.subtract
+                out=shift[:], in0=sum_g[:], scalar=-1.0 / FEAT, in1=line[:, 1, :], op0=ALU.mult, op1=ALU.subtract
             )
             state[("grr", c)] = grr
-            state[("slope", c)] = slope
+            state[("line", c)] = line
             state[("shift", c)] = shift
-            xe_lin = work.tile([P, PACK, FEAT], BF16, name="xe_lin", bufs=2)
-            for s in range(PACK):
-                nc.scalar.activation(
-                    out=xe_lin[:, s, :], in_=e_raw[:, s, :], func=ACT.Copy, scale=edge_mask[:, c, s : s + 1]
-                )
-            xe_grp = work.tile([P, FEAT, PACK], BF16, name="xe_grp", align_bytes=64)
-            regroup(xe_grp, xe_lin)
-            state[("xe_grp", c)] = xe_grp
 
         def apply(c):
             y_raw, grr = state[("y", c)], state[("grr", c)]
-            slope, shift = state[("slope", c)], state[("shift", c)]
+            line, shift = state[("line", c)], state[("shift", c)]
             for s in range(PACK):
                 nc.scalar.activation(
                     out=y_raw[:, s, :], in_=y_raw[:, s, :], func=ACT.Identity,
-                    scale=slope[:, s : s + 1], bias=shift[:, s : s + 1],
+                    scale=line[:, 0, s : s + 1], bias=shift[:, s : s + 1],
                 )
             nc.vector.tensor_tensor(
                 out=grr[:].rearrange("p s f -> p (s f)"),
@@ -192,11 +188,12 @@ def tile_densegatlayer_pb_v_kernel(
             dy_grp = work.tile([P, FEAT, PACK], BF16, name="dy_grp", align_bytes=64)
             regroup(dy_grp, dy)
             state[("dy_grp", c)] = dy_grp
+            b = c // PASSES_PER_GRAPH
             first_of_graph = c % PASSES_PER_GRAPH == 0
             last_of_graph = c % PASSES_PER_GRAPH == PASSES_PER_GRAPH - 1
             if first_of_graph:
                 for s in range(PACK):
-                    state[("cs", c // PASSES_PER_GRAPH, s)] = psum_cs.tile([P, FEAT], F32, name="cs%d" % s)
+                    state[("cs", b, s)] = psum_cs.tile([P, FEAT], F32, name="cs%d" % s)
             rs_ps = psum_rs.tile([P, FEAT], F32, name="rs_ps")
             for s in range(PACK):
                 for k in range(FBLOCKS):
@@ -206,7 +203,7 @@ def tile_densegatlayer_pb_v_kernel(
                         start=(s == 0 and k == 0), stop=(s == PACK - 1 and k == FBLOCKS - 1),
                     )
             for s in range(PACK):
-                cs_ps = state[("cs", c // PASSES_PER_GRAPH, s)]
+                cs_ps = state[("cs", b, s)]
                 for k in range(FBLOCKS):
                     nc.tensor.matmul(
                         out=cs_ps[:, k * P : (k + 1) * P], lhsT=dy[:, s, k * P : (k + 1) * P], rhs=ident[:],
@@ -215,21 +212,13 @@ def tile_densegatlayer_pb_v_kernel(
                     )
             state[("rs", c)] = rs_ps
 
-        def finish(c):
-            g = c % ROUND
-            if g == 0:
-                state["x_codes"] = codes.tile([P, ROUND, FEAT], U32, name="x_codes", align_bytes=64)
-                state["x_scales"] = codes.tile([P, ROUND, FEAT], U8, name="x_scales", align_bytes=64)
-                state["d_codes"] = codes.tile([P, ROUND, FEAT], U32, name="d_codes", align_bytes=64)
-                state["d_scales"] = codes.tile([P, ROUND, FEAT], U8, name="d_scales", align_bytes=64)
-            x_codes, x_scales = state["x_codes"], state["x_scales"]
-            d_codes, d_scales = state["d_codes"], state["d_scales"]
+        def finish_gradient(c):
+            r, h = c // ROUND, c % ROUND
+            if h == 0:
+                state[("d_codes", r)] = codes.tile([P, ROUND, FEAT], U32, name="d_codes", align_bytes=64)
+                state[("d_scales", r)] = codes.tile([P, ROUND, FEAT], U8, name="d_scales", align_bytes=64)
             nc.vector.quantize_mx(
-                out=x_codes[:, g, :].bitcast(E4M3_X4), scales=x_scales[:, g, :],
-                in_=state[("xe_grp", c)][:].rearrange("p f s -> p (f s)"),
-            )
-            nc.vector.quantize_mx(
-                out=d_codes[:, g, :].bitcast(E5M2_X4), scales=d_scales[:, g, :],
+                out=state[("d_codes", r)][:, h, :].bitcast(E5M2_X4), scales=state[("d_scales", r)][:, h, :],
                 in_=state[("dy_grp", c)][:].rearrange("p f s -> p (f s)"),
             )
             nc.vector.tensor_reduce(
@@ -246,48 +235,80 @@ def tile_densegatlayer_pb_v_kernel(
                         in_=state[("cs", b, s)][:].rearrange("p (k i q) -> p k q i", k=FBLOCKS, q=PARTS_PER_ROW),
                         axis=AX.X, op=ALU.add,
                     )
-            if g == ROUND - 1:
-                for m in range(FBLOCKS):
-                    m_cols = slice(m * P, (m + 1) * P)
-                    mx_ps = psum_mx.tile([P, FEAT], F32, name="mx_ps")
-                    for h in range(ROUND):
-                        nc.tensor.matmul_mx(
-                            out=mx_ps[:],
-                            lhsT=x_codes[:, h, m_cols].bitcast(E4M3_X4), lhsT_scale=x_scales[:, h, m_cols],
-                            rhs=d_codes[:, h, :].bitcast(E5M2_X4), rhs_scale=d_scales[:, h, :],
-                            start=(h == 0), stop=(h == ROUND - 1),
-                        )
-                    if c < ROUND:
-                        nc.scalar.copy(out=edge_acc[:, m, :], in_=mx_ps[:])
-                    else:
-                        nc.vector.tensor_tensor(out=edge_acc[:, m, :], in0=mx_ps[:], in1=edge_acc[:, m, :], op=ALU.add)
-                    if c == PASSES - 1:
-                        nc.sync.dma_start(out=out[2 * FEAT + m * P : 2 * FEAT + (m + 1) * P, :], in_=edge_acc[:, m, :])
 
-        load(0)
-        load(1)
-        for step in range(PASSES + 2):
-            if step + 2 < PASSES:
-                load(step + 2)
+        def node_products():
+            for which, sums_t in enumerate((row_sums_t, col_sums_t)):
+                back_ps = psum_rs.tile([P, FEAT], F32, name="rs_ps")
+                for k in range(FBLOCKS):
+                    nc.tensor.transpose(back_ps[:, k * P : (k + 1) * P], sums_t[:, k, :], ident[:])
+                sums = const.tile([P, FEAT], F32, name="sums%d" % which)
+                nc.vector.tensor_copy(out=sums[:], in_=back_ps[:])
+                for m in range(FBLOCKS):
+                    prod_ps = psum_cs.tile([P, FEAT], F32, name="cs%d" % m)
+                    nc.tensor.matmul(
+                        out=prod_ps[:], lhsT=node_f32[:, m * P : (m + 1) * P], rhs=sums[:], start=True, stop=True
+                    )
+                    prod = work.tile([P, FEAT], F32, name="prod")
+                    nc.vector.tensor_copy(out=prod[:], in_=prod_ps[:])
+                    nc.sync.dma_start(out=out[which * FEAT + m * P : which * FEAT + (m + 1) * P, :], in_=prod[:])
+
+        def mask_edges(c):
+            e_raw = state[("e", c)]
+            xe_lin = work.tile([P, PACK, FEAT], BF16, name="xe_lin", bufs=2)
+            for s in range(PACK):
+                nc.scalar.activation(
+                    out=xe_lin[:, s, :], in_=e_raw[:, s, :], func=ACT.Copy, scale=edge_mask[:, c, s : s + 1]
+                )
+            xe_grp = work.tile([P, FEAT, PACK], BF16, name="xe_grp", bufs=2, align_bytes=64)
+            regroup(xe_grp, xe_lin)
+            state[("xe_grp", c)] = xe_grp
+
+        def finish_edges(c):
+            r, h = c // ROUND, c % ROUND
+            if h == 0:
+                state[("x_codes", r)] = codes.tile([P, ROUND, FEAT], U32, name="x_codes", align_bytes=64)
+                state[("x_scales", r)] = codes.tile([P, ROUND, FEAT], U8, name="x_scales", align_bytes=64)
+            x_codes, x_scales = state[("x_codes", r)], state[("x_scales", r)]
+            d_codes, d_scales = state[("d_codes", r)], state[("d_scales", r)]
+            nc.vector.quantize_mx(
+                out=x_codes[:, h, :].bitcast(E4M3_X4), scales=x_scales[:, h, :],
+                in_=state[("xe_grp", c)][:].rearrange("p f s -> p (f s)"),
+            )
+            if h < ROUND - 1:
+                return
+            for m in range(FBLOCKS):
+                m_cols = slice(m * P, (m + 1) * P)
+                mx_ps = psum_mx.tile([P, FEAT], F32, name="mx_ps")
+                for t in range(ROUND):
+                    nc.tensor.matmul_mx(
+                        out=mx_ps[:],
+                        lhsT=x_codes[:, t, m_cols].bitcast(E4M3_X4), lhsT_scale=x_scales[:, t, m_cols],
+                        rhs=d_codes[:, t, :].bitcast(E5M2_X4), rhs_scale=d_scales[:, t, :],
+                        start=(t == 0), stop=(t == ROUND - 1),
+                    )
+                if r == 0:
+                    nc.scalar.copy(out=edge_acc[:, m, :], in_=mx_ps[:])
+                else:
+                    nc.vector.tensor_tensor(out=edge_acc[:, m, :], in0=mx_ps[:], in1=edge_acc[:, m, :], op=ALU.add)
+                if c == PASSES - 1:
+                    nc.sync.dma_start(out=out[2 * FEAT + m * P : 2 * FEAT + (m + 1) * P, :], in_=edge_acc[:, m, :])
+
+        for step in range(PASSES + LAG + 2):
+            if 2 <= step + 2 < PASSES:
+                load_gradient(step + 2)
+            if 0 <= step + 2 - LAG < PASSES:
+                load_edges(step + 2 - LAG)
             if step < PASSES:
                 statistics(step)
-            if 1 <= step <= PASSES:
+            if step == 0:
+                build_edge_mask()
+            if 0 <= step - 1 < PASSES:
                 apply(step - 1)
-            if step >= 2:
-                finish(step - 2)
-
-        for which, sums_t in enumerate((row_sums_t, col_sums_t)):
-            back_ps = psum_rs.tile([P, FEAT], F32, name="rs_ps")
-            for k in range(FBLOCKS):
-                nc.tensor.transpose(back_ps[:, k * P : (k + 1) * P], sums_t[:, k, :], ident[:])
-            sums = const.tile([P, FEAT], F32, name="sums%d" % which)
-            nc.scalar.copy(out=sums[:], in_=back_ps[:])
-            for m in range(FBLOCKS):
-                prod_ps = psum_cs.tile([P, FEAT], F32, name="cs%d" % m)
-                nc.tensor.matmul(out=prod_ps[:], lhsT=node_f32[:, m * P : (m + 1) * P], rhs=sums[:], start=True, stop=True)
-                prod = work.tile([P, FEAT], F32, name="prod")
-                if m % 2 == 0:
-                    nc.scalar.copy(out=prod[:], in_=prod_ps[:])
-                else:
-                    nc.vector.tensor_copy(out=prod[:], in_=prod_ps[:])
-                nc.sync.dma_start(out=out[which * FEAT + m * P : which * FEAT + (m + 1) * P, :], in_=prod[:])
+            if 0 <= step - 2 < PASSES:
+                finish_gradient(step - 2)
+            if step - 2 == PASSES - 1:
+                node_products()
+            if 0 <= step - LAG < PASSES:
+                mask_edges(step - LAG)
+            if 0 <= step - LAG - 1 < PASSES:
+                finish_edges(step - LAG - 1)

@@ -25,7 +25,7 @@ PASSES_PER_GRAPH = PASSES // GRAPHS
 ROWS_PER_PASS = K_PASS // NODES
 PARTS_PER_ROW = P // ROWS_PER_PASS
 FBLOCKS = FEAT // P
-ROUND = 4
+LIVE_TILES = 3
 LAG = 3
 
 FLOPS = 2 * TOKENS * FEAT * FEAT + 2 * 2 * GRAPHS * NODES * FEAT * FEAT
@@ -44,10 +44,9 @@ def tile_densegatlayer_pb_v_kernel(
         loads = ctx.enter_context(tc.tile_pool(name="loads", bufs=3))
         work = ctx.enter_context(tc.tile_pool(name="work", bufs=3))
         small = ctx.enter_context(tc.tile_pool(name="small", bufs=4))
-        codes = ctx.enter_context(tc.tile_pool(name="codes", bufs=2))
         psum_cs = ctx.enter_context(tc.psum_pool(name="psum_cs", bufs=1))
-        psum_rs = ctx.enter_context(tc.psum_pool(name="psum_rs", bufs=2))
-        psum_mx = ctx.enter_context(tc.psum_pool(name="psum_mx", bufs=2))
+        psum_rs = ctx.enter_context(tc.psum_pool(name="psum_rs", bufs=1))
+        psum_mx = ctx.enter_context(tc.psum_pool(name="psum_mx", bufs=1))
 
         state = {}
 
@@ -94,7 +93,11 @@ def tile_densegatlayer_pb_v_kernel(
 
         row_sums_t = const.tile([P, FBLOCKS, P], F32, name="row_sums_t")
         col_sums_t = const.tile([P, FBLOCKS, P], F32, name="col_sums_t")
-        edge_acc = const.tile([P, FBLOCKS, FEAT], F32, name="edge_acc")
+        x_codes = const.tile([P, PASSES, FEAT], U32, name="x_codes", align_bytes=64)
+        x_scales = const.tile([P, PASSES, FEAT], U8, name="x_scales", align_bytes=64)
+        d_codes = const.tile([P, PASSES, FEAT], U32, name="d_codes", align_bytes=64)
+        d_scales = const.tile([P, PASSES, FEAT], U8, name="d_scales", align_bytes=64)
+        live_ps = [psum_mx.tile([P, FEAT], F32, name="mx%d" % m) for m in range(LIVE_TILES)]
         edge_mask = const.tile([P, PASSES, PACK], F32, name="edge_mask")
         node_f32 = const.tile([P, FEAT], F32, name="node_f32")
 
@@ -158,16 +161,24 @@ def tile_densegatlayer_pb_v_kernel(
                     out=junk[:, s, :], in0=y_raw[:, s, :], scalar=mu_t[:, c, s : s + 1], in1=grr[:, s, :],
                     op0=ALU.subtract, op1=ALU.mult, accum_out=sum_gy[:, s : s + 1],
                 )
+            state[("grr", c)] = grr
+            state[("sum_g", c)] = sum_g
+            state[("sum_gy", c)] = sum_gy
+
+        def line_slope(c):
+            sum_gy = state[("sum_gy", c)]
             line = small.tile([P, 2, PACK], F32, name="line")
             nc.vector.tensor_tensor(
                 out=line[:], in0=coef[:, c, :, :], in1=sum_gy[:].unsqueeze(1).to_broadcast([P, 2, PACK]), op=ALU.mult
             )
+            state[("line", c)] = line
+
+        def line_shift(c):
+            sum_g, line = state[("sum_g", c)], state[("line", c)]
             shift = small.tile([P, PACK], F32, name="shift")
             nc.vector.scalar_tensor_tensor(
                 out=shift[:], in0=sum_g[:], scalar=-1.0 / FEAT, in1=line[:, 1, :], op0=ALU.mult, op1=ALU.subtract
             )
-            state[("grr", c)] = grr
-            state[("line", c)] = line
             state[("shift", c)] = shift
 
         def apply(c):
@@ -212,15 +223,13 @@ def tile_densegatlayer_pb_v_kernel(
                     )
             state[("rs", c)] = rs_ps
 
-        def finish_gradient(c):
-            r, h = c // ROUND, c % ROUND
-            if h == 0:
-                state[("d_codes", r)] = codes.tile([P, ROUND, FEAT], U32, name="d_codes", align_bytes=64)
-                state[("d_scales", r)] = codes.tile([P, ROUND, FEAT], U8, name="d_scales", align_bytes=64)
+        def quantise_gradient(c):
             nc.vector.quantize_mx(
-                out=state[("d_codes", r)][:, h, :].bitcast(E5M2_X4), scales=state[("d_scales", r)][:, h, :],
+                out=d_codes[:, c, :].bitcast(E5M2_X4), scales=d_scales[:, c, :],
                 in_=state[("dy_grp", c)][:].rearrange("p f s -> p (f s)"),
             )
+
+        def flush_sums(c):
             nc.vector.tensor_reduce(
                 out=row_sums_t[:, :, c * ROWS_PER_PASS : (c + 1) * ROWS_PER_PASS],
                 in_=state[("rs", c)][:].rearrange("p (k i q) -> p k i q", k=FBLOCKS, q=PARTS_PER_ROW),
@@ -244,7 +253,7 @@ def tile_densegatlayer_pb_v_kernel(
                 sums = const.tile([P, FEAT], F32, name="sums%d" % which)
                 nc.vector.tensor_copy(out=sums[:], in_=back_ps[:])
                 for m in range(FBLOCKS):
-                    prod_ps = psum_cs.tile([P, FEAT], F32, name="cs%d" % m)
+                    prod_ps = psum_cs.tile([P, FEAT], F32, name="cs%d" % (m % (PACK - 1)))
                     nc.tensor.matmul(
                         out=prod_ps[:], lhsT=node_f32[:, m * P : (m + 1) * P], rhs=sums[:], start=True, stop=True
                     )
@@ -263,35 +272,35 @@ def tile_densegatlayer_pb_v_kernel(
             regroup(xe_grp, xe_lin)
             state[("xe_grp", c)] = xe_grp
 
+        def edge_pass(acc, m, c):
+            m_cols = slice(m * P, (m + 1) * P)
+            nc.tensor.matmul_mx(
+                out=acc[:],
+                lhsT=x_codes[:, c, m_cols].bitcast(E4M3_X4), lhsT_scale=x_scales[:, c, m_cols],
+                rhs=d_codes[:, c, :].bitcast(E5M2_X4), rhs_scale=d_scales[:, c, :],
+                start=(c == 0), stop=(c == PASSES - 1),
+            )
+
+        def store_edge_block(acc, m):
+            block = work.tile([P, FEAT], F32, name="prod")
+            nc.vector.tensor_copy(out=block[:], in_=acc[:])
+            nc.sync.dma_start(out=out[2 * FEAT + m * P : 2 * FEAT + (m + 1) * P, :], in_=block[:])
+
         def finish_edges(c):
-            r, h = c // ROUND, c % ROUND
-            if h == 0:
-                state[("x_codes", r)] = codes.tile([P, ROUND, FEAT], U32, name="x_codes", align_bytes=64)
-                state[("x_scales", r)] = codes.tile([P, ROUND, FEAT], U8, name="x_scales", align_bytes=64)
-            x_codes, x_scales = state[("x_codes", r)], state[("x_scales", r)]
-            d_codes, d_scales = state[("d_codes", r)], state[("d_scales", r)]
             nc.vector.quantize_mx(
-                out=x_codes[:, h, :].bitcast(E4M3_X4), scales=x_scales[:, h, :],
+                out=x_codes[:, c, :].bitcast(E4M3_X4), scales=x_scales[:, c, :],
                 in_=state[("xe_grp", c)][:].rearrange("p f s -> p (f s)"),
             )
-            if h < ROUND - 1:
-                return
-            for m in range(FBLOCKS):
-                m_cols = slice(m * P, (m + 1) * P)
-                mx_ps = psum_mx.tile([P, FEAT], F32, name="mx_ps")
-                for t in range(ROUND):
-                    nc.tensor.matmul_mx(
-                        out=mx_ps[:],
-                        lhsT=x_codes[:, t, m_cols].bitcast(E4M3_X4), lhsT_scale=x_scales[:, t, m_cols],
-                        rhs=d_codes[:, t, :].bitcast(E5M2_X4), rhs_scale=d_scales[:, t, :],
-                        start=(t == 0), stop=(t == ROUND - 1),
-                    )
-                if r == 0:
-                    nc.scalar.copy(out=edge_acc[:, m, :], in_=mx_ps[:])
-                else:
-                    nc.vector.tensor_tensor(out=edge_acc[:, m, :], in0=mx_ps[:], in1=edge_acc[:, m, :], op=ALU.add)
-                if c == PASSES - 1:
-                    nc.sync.dma_start(out=out[2 * FEAT + m * P : 2 * FEAT + (m + 1) * P, :], in_=edge_acc[:, m, :])
+            for m in range(LIVE_TILES):
+                edge_pass(live_ps[m], m, c)
+
+        def last_edge_blocks():
+            late_ps = psum_cs.tile([P, FEAT], F32, name="cs%d" % (PACK - 1))
+            for c in range(PASSES):
+                edge_pass(late_ps, LIVE_TILES, c)
+            for m in range(LIVE_TILES):
+                store_edge_block(live_ps[m], m)
+            store_edge_block(late_ps, LIVE_TILES)
 
         for step in range(PASSES + LAG + 2):
             if 2 <= step + 2 < PASSES:
@@ -300,15 +309,22 @@ def tile_densegatlayer_pb_v_kernel(
                 load_edges(step + 2 - LAG)
             if step < PASSES:
                 statistics(step)
+            if 0 <= step - 2 < PASSES:
+                quantise_gradient(step - 2)
+            if step < PASSES:
+                line_slope(step)
+            if 0 <= step - 2 < PASSES:
+                flush_sums(step - 2)
+            if step < PASSES:
+                line_shift(step)
             if step == 0:
                 build_edge_mask()
-            if 0 <= step - 1 < PASSES:
-                apply(step - 1)
-            if 0 <= step - 2 < PASSES:
-                finish_gradient(step - 2)
             if step - 2 == PASSES - 1:
                 node_products()
-            if 0 <= step - LAG < PASSES:
-                mask_edges(step - LAG)
             if 0 <= step - LAG - 1 < PASSES:
                 finish_edges(step - LAG - 1)
+            if 0 <= step - 1 < PASSES:
+                apply(step - 1)
+            if 0 <= step - LAG < PASSES:
+                mask_edges(step - LAG)
+        last_edge_blocks()

@@ -25,7 +25,8 @@ PASSES_PER_GRAPH = PASSES // GRAPHS
 ROWS_PER_PASS = K_PASS // NODES
 PARTS_PER_ROW = P // ROWS_PER_PASS
 FBLOCKS = FEAT // P
-LIVE_TILES = 3
+LIVE_TILES = 2
+VEC_SLOTS = 2
 LAG = 3
 
 FLOPS = 2 * TOKENS * FEAT * FEAT + 2 * 2 * GRAPHS * NODES * FEAT * FEAT
@@ -47,6 +48,7 @@ def tile_densegatlayer_pb_v_kernel(
         psum_cs = ctx.enter_context(tc.psum_pool(name="psum_cs", bufs=1))
         psum_rs = ctx.enter_context(tc.psum_pool(name="psum_rs", bufs=1))
         psum_mx = ctx.enter_context(tc.psum_pool(name="psum_mx", bufs=1))
+        psum_gx = ctx.enter_context(tc.psum_pool(name="psum_gx", bufs=1))
 
         state = {}
 
@@ -67,8 +69,13 @@ def tile_densegatlayer_pb_v_kernel(
             state[("e", c)] = e_raw
 
         load_gradient(0)
-        gamma_bc = const.tile([P, FEAT], BF16, name="gamma_bc")
-        nc.scalar.dma_start(out=gamma_bc[:], in_=gamma_e.partition_broadcast(P))
+        gamma_row = const.tile([P, FEAT], BF16, name="gamma_row")
+        nc.vector.memset(gamma_row[:], 0.0)
+        nc.scalar.dma_start(out=gamma_row[0:1, :], in_=gamma_e.unsqueeze(0))
+        ones = const.tile([P, P], BF16, name="ones")
+        nc.vector.memset(ones[:], 1.0)
+        gamma_ps = psum_gx.tile([P, FEAT], F32, name="gx")
+        nc.tensor.matmul(out=gamma_ps[:], lhsT=ones[:], rhs=gamma_row[:], start=True, stop=True)
         rstd_t = const.tile([P, PASSES, PACK], F32, name="rstd_t")
         nc.scalar.dma_start(
             out=rstd_t[:], in_=rstd.rearrange("b i j -> (b i j)").rearrange("(c p s) -> p c s", p=P, s=PACK)
@@ -97,7 +104,7 @@ def tile_densegatlayer_pb_v_kernel(
         x_scales = const.tile([P, PASSES, FEAT], U8, name="x_scales", align_bytes=64)
         d_codes = const.tile([P, PASSES, FEAT], U32, name="d_codes", align_bytes=64)
         d_scales = const.tile([P, PASSES, FEAT], U8, name="d_scales", align_bytes=64)
-        live_ps = [psum_mx.tile([P, FEAT], F32, name="mx%d" % m) for m in range(LIVE_TILES)]
+        acc_ps = [psum_mx.tile([P, FEAT], F32, name="mx%d" % m) for m in range(LIVE_TILES)]
         edge_mask = const.tile([P, PASSES, PACK], F32, name="edge_mask")
         node_f32 = const.tile([P, FEAT], F32, name="node_f32")
 
@@ -145,24 +152,27 @@ def tile_densegatlayer_pb_v_kernel(
                 in_=src[:].rearrange("p s (c i) -> p c s i", i=4),
             )
 
-        def statistics(c):
-            g_raw, y_raw = state[("g", c)], state[("y", c)]
+        def scaled_gradient(c):
+            g_raw = state[("g", c)]
             grr = work.tile([P, PACK, FEAT], F32, name="grr")
-            junk = work.tile([P, PACK, FEAT], BF16, name="junk", bufs=2)
             sum_g = small.tile([P, PACK], F32, name="sum_g")
-            sum_gy = small.tile([P, PACK], F32, name="sum_gy")
             for s in range(PACK):
                 nc.vector.scalar_tensor_tensor(
-                    out=grr[:, s, :], in0=g_raw[:, s, :], scalar=rstd_t[:, c, s : s + 1], in1=gamma_bc[:],
+                    out=grr[:, s, :], in0=g_raw[:, s, :], scalar=rstd_t[:, c, s : s + 1], in1=gamma_ps[:],
                     op0=ALU.mult, op1=ALU.mult, accum_out=sum_g[:, s : s + 1],
                 )
+            state[("grr", c)] = grr
+            state[("sum_g", c)] = sum_g
+
+        def gradient_dot_y(c):
+            y_raw, grr = state[("y", c)], state[("grr", c)]
+            junk = work.tile([P, PACK, FEAT], BF16, name="junk", bufs=1)
+            sum_gy = small.tile([P, PACK], F32, name="sum_gy")
             for s in range(PACK):
                 nc.vector.scalar_tensor_tensor(
                     out=junk[:, s, :], in0=y_raw[:, s, :], scalar=mu_t[:, c, s : s + 1], in1=grr[:, s, :],
                     op0=ALU.subtract, op1=ALU.mult, accum_out=sum_gy[:, s : s + 1],
                 )
-            state[("grr", c)] = grr
-            state[("sum_g", c)] = sum_g
             state[("sum_gy", c)] = sum_gy
 
         def line_slope(c):
@@ -181,24 +191,36 @@ def tile_densegatlayer_pb_v_kernel(
             )
             state[("shift", c)] = shift
 
-        def apply(c):
-            y_raw, grr = state[("y", c)], state[("grr", c)]
+        def line_of_y(c):
+            y_raw = state[("y", c)]
             line, shift = state[("line", c)], state[("shift", c)]
-            for s in range(PACK):
+            for s in list(range(VEC_SLOTS, PACK)) + list(range(VEC_SLOTS)):
                 nc.scalar.activation(
                     out=y_raw[:, s, :], in_=y_raw[:, s, :], func=ACT.Identity,
                     scale=line[:, 0, s : s + 1], bias=shift[:, s : s + 1],
                 )
+
+        def add_line_on_gpsimd(c):
+            y_raw, grr = state[("y", c)], state[("grr", c)]
+            for s in range(VEC_SLOTS, PACK):
+                nc.gpsimd.tensor_tensor(out=grr[:, s, :], in0=grr[:, s, :], in1=y_raw[:, s, :], op=ALU.add)
+
+        def add_line_on_vector(c):
+            y_raw, grr = state[("y", c)], state[("grr", c)]
             nc.vector.tensor_tensor(
-                out=grr[:].rearrange("p s f -> p (s f)"),
-                in0=grr[:].rearrange("p s f -> p (s f)"),
-                in1=y_raw[:].rearrange("p s f -> p (s f)"),
+                out=grr[:, 0:VEC_SLOTS, :].rearrange("p s f -> p (s f)"),
+                in0=grr[:, 0:VEC_SLOTS, :].rearrange("p s f -> p (s f)"),
+                in1=y_raw[:, 0:VEC_SLOTS, :].rearrange("p s f -> p (s f)"),
                 op=ALU.add,
             )
-            dy = grr
+
+        def regroup_gradient(c):
             dy_grp = work.tile([P, FEAT, PACK], BF16, name="dy_grp", align_bytes=64)
-            regroup(dy_grp, dy)
+            regroup(dy_grp, state[("grr", c)])
             state[("dy_grp", c)] = dy_grp
+
+        def transpose_gradient(c):
+            dy = state[("grr", c)]
             b = c // PASSES_PER_GRAPH
             first_of_graph = c % PASSES_PER_GRAPH == 0
             last_of_graph = c % PASSES_PER_GRAPH == PASSES_PER_GRAPH - 1
@@ -291,24 +313,28 @@ def tile_densegatlayer_pb_v_kernel(
                 out=x_codes[:, c, :].bitcast(E4M3_X4), scales=x_scales[:, c, :],
                 in_=state[("xe_grp", c)][:].rearrange("p f s -> p (f s)"),
             )
-            for m in range(LIVE_TILES):
-                edge_pass(live_ps[m], m, c)
+            for m, acc in enumerate(acc_ps):
+                edge_pass(acc, m, c)
 
-        def last_edge_blocks():
-            late_ps = psum_cs.tile([P, FEAT], F32, name="cs%d" % (PACK - 1))
-            for c in range(PASSES):
-                edge_pass(late_ps, LIVE_TILES, c)
-            for m in range(LIVE_TILES):
-                store_edge_block(live_ps[m], m)
-            store_edge_block(late_ps, LIVE_TILES)
+        def catch_up(acc, passes):
+            m = len(acc_ps)
+            acc_ps.append(acc)
+            for c in passes:
+                edge_pass(acc, m, c)
 
-        for step in range(PASSES + LAG + 2):
+        def one_step(step):
             if 2 <= step + 2 < PASSES:
                 load_gradient(step + 2)
             if 0 <= step + 2 - LAG < PASSES:
                 load_edges(step + 2 - LAG)
             if step < PASSES:
-                statistics(step)
+                scaled_gradient(step)
+            if 0 <= step - 1 < PASSES:
+                add_line_on_gpsimd(step - 1)
+            if step == 0:
+                build_edge_mask()
+            if step < PASSES:
+                gradient_dot_y(step)
             if 0 <= step - 2 < PASSES:
                 quantise_gradient(step - 2)
             if step < PASSES:
@@ -317,14 +343,27 @@ def tile_densegatlayer_pb_v_kernel(
                 flush_sums(step - 2)
             if step < PASSES:
                 line_shift(step)
-            if step == 0:
-                build_edge_mask()
+                line_of_y(step)
             if step - 2 == PASSES - 1:
                 node_products()
             if 0 <= step - LAG - 1 < PASSES:
                 finish_edges(step - LAG - 1)
             if 0 <= step - 1 < PASSES:
-                apply(step - 1)
+                add_line_on_vector(step - 1)
+                regroup_gradient(step - 1)
+                transpose_gradient(step - 1)
+            if step == PASSES:
+                catch_up(psum_gx.tile([P, FEAT], F32, name="gx"), range(step - LAG))
             if 0 <= step - LAG < PASSES:
                 mask_edges(step - LAG)
-        last_edge_blocks()
+
+        with tc.manual_schedule(
+            engines={mybir.EngineType.PE, mybir.EngineType.Activation, mybir.EngineType.DVE, mybir.EngineType.Pool}
+        ):
+            for step in range(PASSES + 1):
+                one_step(step)
+        for step in range(PASSES + 1, PASSES + LAG + 2):
+            one_step(step)
+        catch_up(psum_cs.tile([P, FEAT], F32, name="cs%d" % (PACK - 1)), range(PASSES))
+        for m, acc in enumerate(acc_ps):
+            store_edge_block(acc, m)

@@ -26,6 +26,7 @@ ROWS_PER_PASS = K_PASS // NODES
 PARTS_PER_ROW = P // ROWS_PER_PASS
 FBLOCKS = FEAT // P
 LIVE_TILES = 2
+MASK_VEC_SLOTS = 2
 VEC_SLOTS = 2
 LAG = 3
 
@@ -280,13 +281,18 @@ def tile_densegatlayer_pb_v_kernel(
                         out=prod_ps[:], lhsT=node_f32[:, m * P : (m + 1) * P], rhs=sums[:], start=True, stop=True
                     )
                     prod = work.tile([P, FEAT], F32, name="prod")
-                    nc.vector.tensor_copy(out=prod[:], in_=prod_ps[:])
+                    nc.scalar.copy(out=prod[:], in_=prod_ps[:])
                     nc.sync.dma_start(out=out[which * FEAT + m * P : which * FEAT + (m + 1) * P, :], in_=prod[:])
 
         def mask_edges(c):
             e_raw = state[("e", c)]
             xe_lin = work.tile([P, PACK, FEAT], BF16, name="xe_lin", bufs=2)
-            for s in range(PACK):
+            vec_slots = PACK if c >= PASSES - LAG else MASK_VEC_SLOTS
+            for s in range(vec_slots):
+                nc.vector.tensor_scalar(
+                    out=xe_lin[:, s, :], in0=e_raw[:, s, :], scalar1=edge_mask[:, c, s : s + 1], scalar2=None, op0=ALU.mult
+                )
+            for s in range(vec_slots, PACK):
                 nc.scalar.activation(
                     out=xe_lin[:, s, :], in_=e_raw[:, s, :], func=ACT.Copy, scale=edge_mask[:, c, s : s + 1]
                 )

@@ -22,10 +22,12 @@ TOKENS = GRAPHS * NODES * NODES
 K_PASS = P * PACK
 PASSES = TOKENS // K_PASS
 PASSES_PER_GRAPH = PASSES // GRAPHS
+HEAD_PASSES = 2
 ROWS_PER_PASS = K_PASS // NODES
 PARTS_PER_ROW = P // ROWS_PER_PASS
 FBLOCKS = FEAT // P
 LIVE_TILES = 2
+FIRST_PART = 10
 MASK_VEC_SLOTS = 2
 VEC_SLOTS = 2
 LAG = 3
@@ -46,6 +48,7 @@ def tile_densegatlayer_pb_v_kernel(
         loads = ctx.enter_context(tc.tile_pool(name="loads", bufs=3))
         work = ctx.enter_context(tc.tile_pool(name="work", bufs=3))
         small = ctx.enter_context(tc.tile_pool(name="small", bufs=4))
+        tail = ctx.enter_context(tc.tile_pool(name="tail", bufs=1))
         psum_cs = ctx.enter_context(tc.psum_pool(name="psum_cs", bufs=1))
         psum_rs = ctx.enter_context(tc.psum_pool(name="psum_rs", bufs=1))
         psum_mx = ctx.enter_context(tc.psum_pool(name="psum_mx", bufs=1))
@@ -78,26 +81,33 @@ def tile_densegatlayer_pb_v_kernel(
         gamma_ps = psum_gx.tile([P, FEAT], F32, name="gx")
         nc.tensor.matmul(out=gamma_ps[:], lhsT=ones[:], rhs=gamma_row[:], start=True, stop=True)
         rstd_t = const.tile([P, PASSES, PACK], F32, name="rstd_t")
-        nc.scalar.dma_start(
-            out=rstd_t[:], in_=rstd.rearrange("b i j -> (b i j)").rearrange("(c p s) -> p c s", p=P, s=PACK)
-        )
         mu_t = const.tile([P, PASSES, PACK], F32, name="mu_t")
-        nc.scalar.dma_start(
-            out=mu_t[:], in_=mu.rearrange("b i j -> (b i j)").rearrange("(c p s) -> p c s", p=P, s=PACK)
-        )
+        coef = const.tile([P, PASSES, 2, PACK], F32, name="coef")
+
+        def load_statistics(passes):
+            for tile, saved in ((rstd_t, rstd), (mu_t, mu)):
+                by_pass = saved.rearrange("b i j -> (b i j)").rearrange("(c p s) -> p c s", p=P, s=PACK)
+                nc.scalar.dma_start(out=tile[:, passes, :], in_=by_pass[:, passes, :])
+
+        def build_coefficients(passes):
+            nc.vector.scalar_tensor_tensor(
+                out=coef[:, passes, 0, :], in0=rstd_t[:, passes, :], scalar=-1.0 / FEAT, in1=rstd_t[:, passes, :],
+                op0=ALU.mult, op1=ALU.mult,
+            )
+            nc.vector.tensor_tensor(
+                out=coef[:, passes, 1, :], in0=coef[:, passes, 0, :], in1=mu_t[:, passes, :], op=ALU.mult
+            )
+
+        load_statistics(slice(0, HEAD_PASSES))
         load_gradient(1)
         mask_all = const.tile([P, P], BF16, name="mask_all")
         nc.scalar.dma_start(out=mask_all[:], in_=node_mask.rearrange("b n -> (b n)").partition_broadcast(P))
         node_bf = const.tile([P, FEAT], BF16, name="node_bf")
         nc.scalar.dma_start(out=node_bf[:], in_=new_node.rearrange("b n f -> (b n) f"))
+        load_statistics(slice(HEAD_PASSES, PASSES))
         ident = const.tile([P, P], F32, name="ident")
         make_identity(nc, ident[:])
-
-        coef = const.tile([P, PASSES, 2, PACK], F32, name="coef")
-        nc.vector.scalar_tensor_tensor(
-            out=coef[:, :, 0, :], in0=rstd_t[:], scalar=-1.0 / FEAT, in1=rstd_t[:], op0=ALU.mult, op1=ALU.mult
-        )
-        nc.vector.tensor_tensor(out=coef[:, :, 1, :], in0=coef[:, :, 0, :], in1=mu_t[:], op=ALU.mult)
+        build_coefficients(slice(0, HEAD_PASSES))
 
         row_sums_t = const.tile([P, FBLOCKS, P], F32, name="row_sums_t")
         col_sums_t = const.tile([P, FBLOCKS, P], F32, name="col_sums_t")
@@ -105,11 +115,12 @@ def tile_densegatlayer_pb_v_kernel(
         x_scales = const.tile([P, PASSES, FEAT], U8, name="x_scales", align_bytes=64)
         d_codes = const.tile([P, PASSES, FEAT], U32, name="d_codes", align_bytes=64)
         d_scales = const.tile([P, PASSES, FEAT], U8, name="d_scales", align_bytes=64)
-        acc_ps = [psum_mx.tile([P, FEAT], F32, name="mx%d" % m) for m in range(LIVE_TILES)]
         edge_mask = const.tile([P, PASSES, PACK], F32, name="edge_mask")
         node_f32 = const.tile([P, FEAT], F32, name="node_f32")
+        first_part = const.tile([P, LIVE_TILES, FEAT], F32, name="first_part")
 
         def build_edge_mask():
+            build_coefficients(slice(HEAD_PASSES, PASSES))
             nc.scalar.copy(out=node_f32[:], in_=node_bf[:])
             sel_row = const.tile([P, ROWS_PER_PASS], F32, name="sel_row")
             nc.vector.tensor_reduce(
@@ -147,8 +158,8 @@ def tile_densegatlayer_pb_v_kernel(
                     op=ALU.mult,
                 )
 
-        def regroup(dst, src):
-            nc.scalar.copy(
+        def regroup(copy, dst, src):
+            copy(
                 out=dst[:].rearrange("p (c i) s -> p c s i", i=4),
                 in_=src[:].rearrange("p s (c i) -> p c s i", i=4),
             )
@@ -206,18 +217,18 @@ def tile_densegatlayer_pb_v_kernel(
             for s in range(VEC_SLOTS, PACK):
                 nc.gpsimd.tensor_tensor(out=grr[:, s, :], in0=grr[:, s, :], in1=y_raw[:, s, :], op=ALU.add)
 
-        def add_line_on_vector(c):
+        def add_line_on_vector(c, slots):
             y_raw, grr = state[("y", c)], state[("grr", c)]
             nc.vector.tensor_tensor(
-                out=grr[:, 0:VEC_SLOTS, :].rearrange("p s f -> p (s f)"),
-                in0=grr[:, 0:VEC_SLOTS, :].rearrange("p s f -> p (s f)"),
-                in1=y_raw[:, 0:VEC_SLOTS, :].rearrange("p s f -> p (s f)"),
+                out=grr[:, 0:slots, :].rearrange("p s f -> p (s f)"),
+                in0=grr[:, 0:slots, :].rearrange("p s f -> p (s f)"),
+                in1=y_raw[:, 0:slots, :].rearrange("p s f -> p (s f)"),
                 op=ALU.add,
             )
 
         def regroup_gradient(c):
             dy_grp = work.tile([P, FEAT, PACK], BF16, name="dy_grp", align_bytes=64)
-            regroup(dy_grp, state[("grr", c)])
+            regroup(nc.scalar.copy, dy_grp, state[("grr", c)])
             state[("dy_grp", c)] = dy_grp
 
         def transpose_gradient(c):
@@ -252,41 +263,38 @@ def tile_densegatlayer_pb_v_kernel(
                 in_=state[("dy_grp", c)][:].rearrange("p f s -> p (f s)"),
             )
 
-        def flush_sums(c):
+        def flush_row_sums(c):
             nc.vector.tensor_reduce(
                 out=row_sums_t[:, :, c * ROWS_PER_PASS : (c + 1) * ROWS_PER_PASS],
                 in_=state[("rs", c)][:].rearrange("p (k i q) -> p k i q", k=FBLOCKS, q=PARTS_PER_ROW),
                 axis=AX.X, op=ALU.add,
             )
-            if c % PASSES_PER_GRAPH == PASSES_PER_GRAPH - 1:
-                b = c // PASSES_PER_GRAPH
-                graph_cols = col_sums_t[:, :, b * NODES : (b + 1) * NODES].rearrange("p k (q s) -> p k q s", s=PACK)
-                for s in range(PACK):
-                    nc.vector.tensor_reduce(
-                        out=graph_cols[:, :, :, s],
-                        in_=state[("cs", b, s)][:].rearrange("p (k i q) -> p k q i", k=FBLOCKS, q=PARTS_PER_ROW),
-                        axis=AX.X, op=ALU.add,
-                    )
 
-        def node_products():
-            for which, sums_t in enumerate((row_sums_t, col_sums_t)):
-                back_ps = psum_rs.tile([P, FEAT], F32, name="rs_ps")
-                for k in range(FBLOCKS):
-                    nc.tensor.transpose(back_ps[:, k * P : (k + 1) * P], sums_t[:, k, :], ident[:])
-                sums = const.tile([P, FEAT], F32, name="sums%d" % which)
-                nc.vector.tensor_copy(out=sums[:], in_=back_ps[:])
-                for m in range(FBLOCKS):
-                    prod_ps = psum_cs.tile([P, FEAT], F32, name="cs%d" % (m % (PACK - 1)))
-                    nc.tensor.matmul(
-                        out=prod_ps[:], lhsT=node_f32[:, m * P : (m + 1) * P], rhs=sums[:], start=True, stop=True
-                    )
-                    prod = work.tile([P, FEAT], F32, name="prod")
-                    nc.scalar.copy(out=prod[:], in_=prod_ps[:])
-                    nc.sync.dma_start(out=out[which * FEAT + m * P : which * FEAT + (m + 1) * P, :], in_=prod[:])
+        def flush_col_sums(b):
+            graph_cols = col_sums_t[:, :, b * NODES : (b + 1) * NODES].rearrange("p k (q s) -> p k q s", s=PACK)
+            for s in range(PACK):
+                nc.vector.tensor_reduce(
+                    out=graph_cols[:, :, :, s],
+                    in_=state[("cs", b, s)][:].rearrange("p (k i q) -> p k q i", k=FBLOCKS, q=PARTS_PER_ROW),
+                    axis=AX.X, op=ALU.add,
+                )
+
+        def turn_sums(sums_t, back_ps):
+            for k in range(FBLOCKS):
+                nc.tensor.transpose(back_ps[:, k * P : (k + 1) * P], sums_t[:, k, :], ident[:])
+            sums = tail.tile([P, FEAT], F32, name="sums", bufs=2)
+            nc.scalar.copy(out=sums[:], in_=back_ps[:])
+            return sums
+
+        def node_product(first_row, m, sums, prod_ps):
+            nc.tensor.matmul(out=prod_ps[:], lhsT=node_f32[:, m * P : (m + 1) * P], rhs=sums[:], start=True, stop=True)
+            prod = tail.tile([P, FEAT], F32, name="prod", bufs=6)
+            nc.scalar.copy(out=prod[:], in_=prod_ps[:])
+            nc.sync.dma_start(out=out[first_row + m * P : first_row + (m + 1) * P, :], in_=prod[:])
 
         def mask_edges(c):
             e_raw = state[("e", c)]
-            xe_lin = work.tile([P, PACK, FEAT], BF16, name="xe_lin", bufs=2)
+            xe_lin = work.tile([P, PACK, FEAT], BF16, name="xe_lin", bufs=3)
             vec_slots = PACK if c >= PASSES - LAG else MASK_VEC_SLOTS
             for s in range(vec_slots):
                 nc.vector.tensor_scalar(
@@ -296,80 +304,138 @@ def tile_densegatlayer_pb_v_kernel(
                 nc.scalar.activation(
                     out=xe_lin[:, s, :], in_=e_raw[:, s, :], func=ACT.Copy, scale=edge_mask[:, c, s : s + 1]
                 )
+            state[("xe", c)] = xe_lin
+
+        def regroup_edges(c, copy):
+            xe_lin = state[("xe", c)]
             xe_grp = work.tile([P, FEAT, PACK], BF16, name="xe_grp", bufs=2, align_bytes=64)
-            regroup(xe_grp, xe_lin)
+            regroup(copy, xe_grp, xe_lin)
             state[("xe_grp", c)] = xe_grp
 
-        def edge_pass(acc, m, c):
+        def edge_pass(acc, m, c, first, last):
             m_cols = slice(m * P, (m + 1) * P)
             nc.tensor.matmul_mx(
                 out=acc[:],
                 lhsT=x_codes[:, c, m_cols].bitcast(E4M3_X4), lhsT_scale=x_scales[:, c, m_cols],
                 rhs=d_codes[:, c, :].bitcast(E5M2_X4), rhs_scale=d_scales[:, c, :],
-                start=(c == 0), stop=(c == PASSES - 1),
+                start=first, stop=last,
             )
 
-        def store_edge_block(acc, m):
-            block = work.tile([P, FEAT], F32, name="prod")
-            nc.vector.tensor_copy(out=block[:], in_=acc[:])
-            nc.sync.dma_start(out=out[2 * FEAT + m * P : 2 * FEAT + (m + 1) * P, :], in_=block[:])
-
-        def finish_edges(c):
+        def quantise_edges(c):
             nc.vector.quantize_mx(
                 out=x_codes[:, c, :].bitcast(E4M3_X4), scales=x_scales[:, c, :],
                 in_=state[("xe_grp", c)][:].rearrange("p f s -> p (f s)"),
             )
-            for m, acc in enumerate(acc_ps):
-                edge_pass(acc, m, c)
 
-        def catch_up(acc, passes):
-            m = len(acc_ps)
-            acc_ps.append(acc)
+        def multiply_edges(c):
+            if c == 0 or c == FIRST_PART:
+                state["acc"] = [psum_mx.tile([P, FEAT], F32, name="mx%d" % m) for m in range(LIVE_TILES)]
+            if c < FIRST_PART:
+                for m, acc in enumerate(state["acc"]):
+                    edge_pass(acc, m, c, c == 0, c == FIRST_PART - 1)
+                if c == FIRST_PART - 1:
+                    for m, acc in enumerate(state["acc"]):
+                        nc.scalar.copy(out=first_part[:, m, :], in_=acc[:])
+            else:
+                missed = FIRST_PART // 2
+                caught_up = range((c - FIRST_PART) * missed, min((c - FIRST_PART + 1) * missed, FIRST_PART))
+                for m, acc in enumerate(state["acc"]):
+                    for past in caught_up:
+                        edge_pass(acc, LIVE_TILES + m, past, past == 0, False)
+                    edge_pass(acc, LIVE_TILES + m, c, False, c == PASSES - 1)
+
+        def multiply_late(acc, m, passes):
             for c in passes:
-                edge_pass(acc, m, c)
+                edge_pass(acc, m, c, c == FIRST_PART, c == PASSES - 1)
+
+        def store_edge_block(m, acc, add=None):
+            block = tail.tile([P, FEAT], F32, name="prod", bufs=6)
+            if add is None:
+                nc.vector.tensor_copy(out=block[:], in_=acc[:])
+            else:
+                nc.vector.tensor_tensor(out=block[:], in0=acc[:], in1=add, op=ALU.add)
+            nc.sync.dma_start(out=out[2 * FEAT + m * P : 2 * FEAT + (m + 1) * P, :], in_=block[:])
 
         def one_step(step):
-            if 2 <= step + 2 < PASSES:
+            if step + 2 < PASSES:
                 load_gradient(step + 2)
-            if 0 <= step + 2 - LAG < PASSES:
+            if 0 <= step + 2 - LAG:
                 load_edges(step + 2 - LAG)
-            if step < PASSES:
-                scaled_gradient(step)
-            if 0 <= step - 1 < PASSES:
+            scaled_gradient(step)
+            if step >= 1:
                 add_line_on_gpsimd(step - 1)
             if step == 0:
                 build_edge_mask()
-            if step < PASSES:
-                gradient_dot_y(step)
-            if 0 <= step - 2 < PASSES:
+            gradient_dot_y(step)
+            if step >= 2:
                 quantise_gradient(step - 2)
-            if step < PASSES:
-                line_slope(step)
-            if 0 <= step - 2 < PASSES:
-                flush_sums(step - 2)
-            if step < PASSES:
-                line_shift(step)
-                line_of_y(step)
-            if step - 2 == PASSES - 1:
-                node_products()
-            if 0 <= step - LAG - 1 < PASSES:
-                finish_edges(step - LAG - 1)
-            if 0 <= step - 1 < PASSES:
-                add_line_on_vector(step - 1)
+            line_slope(step)
+            if step >= 2:
+                flush_row_sums(step - 2)
+                if step - 2 == PASSES_PER_GRAPH - 1:
+                    flush_col_sums(0)
+            line_shift(step)
+            line_of_y(step)
+            if step >= LAG + 1:
+                quantise_edges(step - LAG - 1)
+                multiply_edges(step - LAG - 1)
+            if step >= 1:
+                add_line_on_vector(step - 1, VEC_SLOTS)
                 regroup_gradient(step - 1)
                 transpose_gradient(step - 1)
-            if step == PASSES:
-                catch_up(psum_gx.tile([P, FEAT], F32, name="gx"), range(step - LAG))
-            if 0 <= step - LAG < PASSES:
+            if step >= LAG:
                 mask_edges(step - LAG)
+                regroup_edges(step - LAG, nc.scalar.copy)
+
+        def last_steps():
+            last = PASSES - 1
+            load_edges(last)
+            late0_ps = psum_gx.tile([P, FEAT], F32, name="gx")
+            multiply_late(late0_ps, 0, range(FIRST_PART, last - 3))
+            add_line_on_vector(last, PACK)
+            transpose_gradient(last)
+            quantise_gradient(last - 1)
+            flush_row_sums(last - 1)
+            mask_edges(last - 2)
+            regroup_gradient(last)
+            flush_row_sums(last)
+            row_sums = turn_sums(row_sums_t, psum_rs.tile([P, FEAT], F32, name="rs_ps"))
+            quantise_edges(last - 3)
+            multiply_edges(last - 3)
+            flush_col_sums(1)
+            regroup_edges(last - 2, nc.vector.tensor_copy)
+            node_product(0, 0, row_sums, psum_cs.tile([P, FEAT], F32, name="cs1"))
+            node_product(0, 1, row_sums, psum_cs.tile([P, FEAT], F32, name="cs2"))
+            mask_edges(last - 1)
+            quantise_gradient(last)
+            quantise_edges(last - 2)
+            col_sums = turn_sums(col_sums_t, psum_cs.tile([P, FEAT], F32, name="cs0"))
+            node_product(0, 2, row_sums, psum_cs.tile([P, FEAT], F32, name="cs1"))
+            node_product(0, 3, row_sums, psum_cs.tile([P, FEAT], F32, name="cs2"))
+            multiply_edges(last - 2)
+            late1_ps = psum_rs.tile([P, FEAT], F32, name="rs_ps")
+            multiply_late(late1_ps, 1, range(FIRST_PART, last - 1))
+            multiply_late(late0_ps, 0, range(last - 3, last - 1))
+            regroup_edges(last - 1, nc.vector.tensor_copy)
+            mask_edges(last)
+            quantise_edges(last - 1)
+            regroup_edges(last, nc.vector.tensor_copy)
+            node_product(FEAT, 0, col_sums, psum_cs.tile([P, FEAT], F32, name="cs1"))
+            node_product(FEAT, 1, col_sums, psum_cs.tile([P, FEAT], F32, name="cs2"))
+            multiply_edges(last - 1)
+            quantise_edges(last)
+            node_product(FEAT, 2, col_sums, psum_cs.tile([P, FEAT], F32, name="cs1"))
+            multiply_edges(last)
+            for m, acc in enumerate(state["acc"]):
+                store_edge_block(LIVE_TILES + m, acc)
+            node_product(FEAT, 3, col_sums, psum_cs.tile([P, FEAT], F32, name="cs2"))
+            for m, acc in enumerate((late0_ps, late1_ps)):
+                multiply_late(acc, m, range(last - 1, PASSES))
+                store_edge_block(m, acc, first_part[:, m, :])
 
         with tc.manual_schedule(
             engines={mybir.EngineType.PE, mybir.EngineType.Activation, mybir.EngineType.DVE, mybir.EngineType.Pool}
         ):
-            for step in range(PASSES + 1):
+            for step in range(PASSES):
                 one_step(step)
-        for step in range(PASSES + 1, PASSES + LAG + 2):
-            one_step(step)
-        catch_up(psum_cs.tile([P, FEAT], F32, name="cs%d" % (PACK - 1)), range(PASSES))
-        for m, acc in enumerate(acc_ps):
-            store_edge_block(acc, m)
+            last_steps()

@@ -27,7 +27,8 @@ ROWS_PER_PASS = K_PASS // NODES
 PARTS_PER_ROW = P // ROWS_PER_PASS
 FBLOCKS = FEAT // P
 LIVE_TILES = 2
-FIRST_PART = 10
+FIRST_PART = 9
+SLOT_ORDER = (2, 3, 0, 1)
 MASK_VEC_SLOTS = 2
 VEC_SLOTS = 2
 LAG = 3
@@ -72,10 +73,9 @@ def tile_densegatlayer_pb_v_kernel(
             nc.sync.dma_start(out=e_raw[:], in_=pass_rows(emb_rows, c))
             state[("e", c)] = e_raw
 
-        load_gradient(0)
         gamma_row = const.tile([P, FEAT], BF16, name="gamma_row")
         nc.vector.memset(gamma_row[:], 0.0)
-        nc.scalar.dma_start(out=gamma_row[0:1, :], in_=gamma_e.unsqueeze(0))
+        nc.sync.dma_start(out=gamma_row[0:1, :], in_=gamma_e.unsqueeze(0))
         ones = const.tile([P, P], BF16, name="ones")
         nc.vector.memset(ones[:], 1.0)
         gamma_ps = psum_gx.tile([P, FEAT], F32, name="gx")
@@ -84,10 +84,10 @@ def tile_densegatlayer_pb_v_kernel(
         mu_t = const.tile([P, PASSES, PACK], F32, name="mu_t")
         coef = const.tile([P, PASSES, 2, PACK], F32, name="coef")
 
-        def load_statistics(passes):
+        def load_statistics(queue, passes):
             for tile, saved in ((rstd_t, rstd), (mu_t, mu)):
                 by_pass = saved.rearrange("b i j -> (b i j)").rearrange("(c p s) -> p c s", p=P, s=PACK)
-                nc.scalar.dma_start(out=tile[:, passes, :], in_=by_pass[:, passes, :])
+                queue.dma_start(out=tile[:, passes, :], in_=by_pass[:, passes, :])
 
         def build_coefficients(passes):
             nc.vector.scalar_tensor_tensor(
@@ -98,13 +98,14 @@ def tile_densegatlayer_pb_v_kernel(
                 out=coef[:, passes, 1, :], in0=coef[:, passes, 0, :], in1=mu_t[:, passes, :], op=ALU.mult
             )
 
-        load_statistics(slice(0, HEAD_PASSES))
+        load_statistics(nc.sync, slice(0, HEAD_PASSES))
+        load_gradient(0)
         load_gradient(1)
         mask_all = const.tile([P, P], BF16, name="mask_all")
         nc.scalar.dma_start(out=mask_all[:], in_=node_mask.rearrange("b n -> (b n)").partition_broadcast(P))
         node_bf = const.tile([P, FEAT], BF16, name="node_bf")
         nc.scalar.dma_start(out=node_bf[:], in_=new_node.rearrange("b n f -> (b n) f"))
-        load_statistics(slice(HEAD_PASSES, PASSES))
+        load_statistics(nc.sync, slice(HEAD_PASSES, PASSES))
         ident = const.tile([P, P], F32, name="ident")
         make_identity(nc, ident[:])
         build_coefficients(slice(0, HEAD_PASSES))
@@ -119,27 +120,28 @@ def tile_densegatlayer_pb_v_kernel(
         node_f32 = const.tile([P, FEAT], F32, name="node_f32")
         first_part = const.tile([P, LIVE_TILES, FEAT], F32, name="first_part")
 
-        def build_edge_mask():
-            build_coefficients(slice(HEAD_PASSES, PASSES))
-            nc.scalar.copy(out=node_f32[:], in_=node_bf[:])
-            sel_row = const.tile([P, ROWS_PER_PASS], F32, name="sel_row")
+        sel_row = const.tile([P, ROWS_PER_PASS], F32, name="sel_row")
+        sel_col = const.tile([P, PARTS_PER_ROW], F32, name="sel_col")
+        pick_i = const.tile([P, PASSES, ROWS_PER_PASS], F32, name="pick_i")
+        pick_j = const.tile([P, GRAPHS * PACK, PARTS_PER_ROW], F32, name="pick_j")
+        mask_i = const.tile([P, PASSES], F32, name="mask_i")
+        mask_j = const.tile([P, GRAPHS * PACK], F32, name="mask_j")
+
+        def build_selectors():
             nc.vector.tensor_reduce(
                 out=sel_row[:], in_=ident[:].rearrange("p (g q) -> p g q", q=PARTS_PER_ROW), axis=AX.X, op=ALU.add
             )
-            sel_col = const.tile([P, PARTS_PER_ROW], F32, name="sel_col")
             nc.vector.tensor_reduce(
                 out=sel_col[:], in_=ident[:].rearrange("p (g q) -> p q g", q=PARTS_PER_ROW), axis=AX.X, op=ALU.add
             )
-            pick_i = const.tile([P, PASSES, ROWS_PER_PASS], F32, name="pick_i")
+
+        def pick_masks():
             nc.vector.tensor_tensor(
                 out=pick_i[:],
                 in0=mask_all[:].rearrange("p (c g) -> p c g", g=ROWS_PER_PASS),
                 in1=sel_row[:].unsqueeze(1).to_broadcast([P, PASSES, ROWS_PER_PASS]),
                 op=ALU.mult,
             )
-            mask_i = const.tile([P, PASSES], F32, name="mask_i")
-            nc.vector.tensor_reduce(out=mask_i[:], in_=pick_i[:], axis=AX.X, op=ALU.add)
-            pick_j = const.tile([P, GRAPHS * PACK, PARTS_PER_ROW], F32, name="pick_j")
             for b in range(GRAPHS):
                 nc.vector.tensor_tensor(
                     out=pick_j[:, b * PACK : (b + 1) * PACK, :],
@@ -147,8 +149,12 @@ def tile_densegatlayer_pb_v_kernel(
                     in1=sel_col[:].unsqueeze(1).to_broadcast([P, PACK, PARTS_PER_ROW]),
                     op=ALU.mult,
                 )
-            mask_j = const.tile([P, GRAPHS * PACK], F32, name="mask_j")
+
+        def reduce_masks():
+            nc.vector.tensor_reduce(out=mask_i[:], in_=pick_i[:], axis=AX.X, op=ALU.add)
             nc.vector.tensor_reduce(out=mask_j[:], in_=pick_j[:], axis=AX.X, op=ALU.add)
+
+        def multiply_masks():
             for b in range(GRAPHS):
                 graph_passes = slice(b * PASSES_PER_GRAPH, (b + 1) * PASSES_PER_GRAPH)
                 nc.vector.tensor_tensor(
@@ -203,10 +209,10 @@ def tile_densegatlayer_pb_v_kernel(
             )
             state[("shift", c)] = shift
 
-        def line_of_y(c):
+        def line_of_y(c, slots):
             y_raw = state[("y", c)]
             line, shift = state[("line", c)], state[("shift", c)]
-            for s in list(range(VEC_SLOTS, PACK)) + list(range(VEC_SLOTS)):
+            for s in slots:
                 nc.scalar.activation(
                     out=y_raw[:, s, :], in_=y_raw[:, s, :], func=ACT.Identity,
                     scale=line[:, 0, s : s + 1], bias=shift[:, s : s + 1],
@@ -217,12 +223,21 @@ def tile_densegatlayer_pb_v_kernel(
             for s in range(VEC_SLOTS, PACK):
                 nc.gpsimd.tensor_tensor(out=grr[:, s, :], in0=grr[:, s, :], in1=y_raw[:, s, :], op=ALU.add)
 
+        def line_of_y_on_vector(c, slots):
+            y_raw = state[("y", c)]
+            line, shift = state[("line", c)], state[("shift", c)]
+            for s in slots:
+                nc.vector.tensor_scalar(
+                    out=y_raw[:, s, :], in0=y_raw[:, s, :],
+                    scalar1=line[:, 0, s : s + 1], scalar2=shift[:, s : s + 1], op0=ALU.mult, op1=ALU.add,
+                )
+
         def add_line_on_vector(c, slots):
             y_raw, grr = state[("y", c)], state[("grr", c)]
             nc.vector.tensor_tensor(
-                out=grr[:, 0:slots, :].rearrange("p s f -> p (s f)"),
-                in0=grr[:, 0:slots, :].rearrange("p s f -> p (s f)"),
-                in1=y_raw[:, 0:slots, :].rearrange("p s f -> p (s f)"),
+                out=grr[:, slots, :].rearrange("p s f -> p (s f)"),
+                in0=grr[:, slots, :].rearrange("p s f -> p (s f)"),
+                in1=y_raw[:, slots, :].rearrange("p s f -> p (s f)"),
                 op=ALU.add,
             )
 
@@ -231,7 +246,19 @@ def tile_densegatlayer_pb_v_kernel(
             regroup(nc.scalar.copy, dy_grp, state[("grr", c)])
             state[("dy_grp", c)] = dy_grp
 
-        def transpose_gradient(c):
+        def transpose_for_row_sums(c):
+            dy = state[("grr", c)]
+            rs_ps = psum_rs.tile([P, FEAT], F32, name="rs_ps")
+            for n, s in enumerate(SLOT_ORDER):
+                for k in range(FBLOCKS):
+                    nc.tensor.matmul(
+                        out=rs_ps[:, k * P : (k + 1) * P], lhsT=dy[:, s, k * P : (k + 1) * P], rhs=ident[:],
+                        is_transpose=True,
+                        start=(n == 0 and k == 0), stop=(n == PACK - 1 and k == FBLOCKS - 1),
+                    )
+            state[("rs", c)] = rs_ps
+
+        def transpose_for_col_sums(c):
             dy = state[("grr", c)]
             b = c // PASSES_PER_GRAPH
             first_of_graph = c % PASSES_PER_GRAPH == 0
@@ -239,15 +266,7 @@ def tile_densegatlayer_pb_v_kernel(
             if first_of_graph:
                 for s in range(PACK):
                     state[("cs", b, s)] = psum_cs.tile([P, FEAT], F32, name="cs%d" % s)
-            rs_ps = psum_rs.tile([P, FEAT], F32, name="rs_ps")
-            for s in range(PACK):
-                for k in range(FBLOCKS):
-                    nc.tensor.matmul(
-                        out=rs_ps[:, k * P : (k + 1) * P], lhsT=dy[:, s, k * P : (k + 1) * P], rhs=ident[:],
-                        is_transpose=True,
-                        start=(s == 0 and k == 0), stop=(s == PACK - 1 and k == FBLOCKS - 1),
-                    )
-            for s in range(PACK):
+            for s in SLOT_ORDER:
                 cs_ps = state[("cs", b, s)]
                 for k in range(FBLOCKS):
                     nc.tensor.matmul(
@@ -255,7 +274,6 @@ def tile_densegatlayer_pb_v_kernel(
                         is_transpose=True,
                         start=(first_of_graph and k == 0), stop=(last_of_graph and k == FBLOCKS - 1),
                     )
-            state[("rs", c)] = rs_ps
 
         def quantise_gradient(c):
             nc.vector.quantize_mx(
@@ -337,7 +355,7 @@ def tile_densegatlayer_pb_v_kernel(
                     for m, acc in enumerate(state["acc"]):
                         nc.scalar.copy(out=first_part[:, m, :], in_=acc[:])
             else:
-                missed = FIRST_PART // 2
+                missed = (FIRST_PART + 1) // 2
                 caught_up = range((c - FIRST_PART) * missed, min((c - FIRST_PART + 1) * missed, FIRST_PART))
                 for m, acc in enumerate(state["acc"]):
                     for past in caught_up:
@@ -361,46 +379,65 @@ def tile_densegatlayer_pb_v_kernel(
                 load_gradient(step + 2)
             if 0 <= step + 2 - LAG:
                 load_edges(step + 2 - LAG)
+            if step == 0:
+                build_selectors()
             scaled_gradient(step)
+            if step == 0:
+                pick_masks()
+                reduce_masks()
+                nc.scalar.copy(out=node_f32[:], in_=node_bf[:])
             if step >= 1:
                 add_line_on_gpsimd(step - 1)
-            if step == 0:
-                build_edge_mask()
+                add_line_on_vector(step - 1, slice(0, VEC_SLOTS))
             gradient_dot_y(step)
-            if step >= 2:
-                quantise_gradient(step - 2)
+            if step == 0:
+                multiply_masks()
+            if step == 1:
+                build_coefficients(slice(HEAD_PASSES, PASSES))
+            if step >= LAG:
+                mask_edges(step - LAG)
             line_slope(step)
             if step >= 2:
                 flush_row_sums(step - 2)
                 if step - 2 == PASSES_PER_GRAPH - 1:
                     flush_col_sums(0)
             line_shift(step)
-            line_of_y(step)
+            line_of_y(step, SLOT_ORDER if step < PASSES - 1 else SLOT_ORDER[VEC_SLOTS:])
+            if step >= 1:
+                regroup_gradient(step - 1)
+                transpose_for_col_sums(step - 1)
+                if step == PASSES - 1:
+                    state["late"] = psum_gx.tile([P, FEAT], F32, name="gx")
+                    multiply_late(state["late"], 0, range(FIRST_PART, step - LAG - 1))
+                transpose_for_row_sums(step - 1)
+            if step == PASSES - 1:
+                line_of_y_on_vector(step, SLOT_ORDER[:VEC_SLOTS])
+                flush_row_sums(step - 1)
+                add_line_on_vector(step, slice(VEC_SLOTS, PACK))
+                add_line_on_vector(step, slice(0, VEC_SLOTS))
+            if step >= 2:
+                quantise_gradient(step - 2)
             if step >= LAG + 1:
                 quantise_edges(step - LAG - 1)
-                multiply_edges(step - LAG - 1)
-            if step >= 1:
-                add_line_on_vector(step - 1, VEC_SLOTS)
-                regroup_gradient(step - 1)
-                transpose_gradient(step - 1)
+                if step < PASSES - 1:
+                    multiply_edges(step - LAG - 1)
             if step >= LAG:
-                mask_edges(step - LAG)
                 regroup_edges(step - LAG, nc.scalar.copy)
 
         def last_steps():
             last = PASSES - 1
             load_edges(last)
-            late0_ps = psum_gx.tile([P, FEAT], F32, name="gx")
-            multiply_late(late0_ps, 0, range(FIRST_PART, last - 3))
-            add_line_on_vector(last, PACK)
-            transpose_gradient(last)
-            quantise_gradient(last - 1)
-            flush_row_sums(last - 1)
-            mask_edges(last - 2)
+            transpose_for_row_sums(last)
+            transpose_for_col_sums(last)
             regroup_gradient(last)
+            mask_edges(last - 2)
+            quantise_gradient(last - 1)
             flush_row_sums(last)
             row_sums = turn_sums(row_sums_t, psum_rs.tile([P, FEAT], F32, name="rs_ps"))
             quantise_edges(last - 3)
+            late0_ps = state["late"]
+            multiply_edges(last - 4)
+            multiply_late(late0_ps, 0, range(last - 4, last - 3))
             multiply_edges(last - 3)
             flush_col_sums(1)
             regroup_edges(last - 2, nc.vector.tensor_copy)

@@ -22,12 +22,12 @@ TOKENS = GRAPHS * NODES * NODES
 K_PASS = P * PACK
 PASSES = TOKENS // K_PASS
 PASSES_PER_GRAPH = PASSES // GRAPHS
-HEAD_PASSES = 2
 ROWS_PER_PASS = K_PASS // NODES
 PARTS_PER_ROW = P // ROWS_PER_PASS
 FBLOCKS = FEAT // P
 LIVE_TILES = 2
-FIRST_PART = 9
+FIRST_PART = 10
+CATCH_UP_STEPS = 2
 SLOT_ORDER = (2, 3, 0, 1)
 MASK_VEC_SLOTS = 2
 VEC_SLOTS = 2
@@ -63,7 +63,7 @@ def tile_densegatlayer_pb_v_kernel(
         def load_gradient(c):
             g_raw = loads.tile([P, PACK, FEAT], BF16, name="g_raw")
             nc.sync.dma_start(out=g_raw[:], in_=pass_rows(grad_rows, c))
-            y_raw = loads.tile([P, PACK, FEAT], F32, name="y_raw", bufs=4)
+            y_raw = loads.tile([P, PACK, FEAT], F32, name="y_raw", bufs=5)
             nc.sync.dma_start(out=y_raw[:], in_=pass_rows(y_rows, c))
             state[("g", c)] = g_raw
             state[("y", c)] = y_raw
@@ -73,42 +73,49 @@ def tile_densegatlayer_pb_v_kernel(
             nc.sync.dma_start(out=e_raw[:], in_=pass_rows(emb_rows, c))
             state[("e", c)] = e_raw
 
-        gamma_row = const.tile([P, FEAT], BF16, name="gamma_row")
-        nc.vector.memset(gamma_row[:], 0.0)
-        nc.sync.dma_start(out=gamma_row[0:1, :], in_=gamma_e.unsqueeze(0))
         ones = const.tile([P, P], BF16, name="ones")
         nc.vector.memset(ones[:], 1.0)
-        gamma_ps = psum_gx.tile([P, FEAT], F32, name="gx")
-        nc.tensor.matmul(out=gamma_ps[:], lhsT=ones[:], rhs=gamma_row[:], start=True, stop=True)
-        rstd_t = const.tile([P, PASSES, PACK], F32, name="rstd_t")
-        mu_t = const.tile([P, PASSES, PACK], F32, name="mu_t")
-        coef = const.tile([P, PASSES, 2, PACK], F32, name="coef")
-
-        def load_statistics(queue, passes):
-            for tile, saved in ((rstd_t, rstd), (mu_t, mu)):
-                by_pass = saved.rearrange("b i j -> (b i j)").rearrange("(c p s) -> p c s", p=P, s=PACK)
-                queue.dma_start(out=tile[:, passes, :], in_=by_pass[:, passes, :])
-
-        def build_coefficients(passes):
-            nc.vector.scalar_tensor_tensor(
-                out=coef[:, passes, 0, :], in0=rstd_t[:, passes, :], scalar=-1.0 / FEAT, in1=rstd_t[:, passes, :],
-                op0=ALU.mult, op1=ALU.mult,
+        small_rows = const.tile([P, FEAT + P], BF16, name="small_rows")
+        nc.vector.memset(small_rows[:], 0.0)
+        stat_rows = const.tile([P, K_PASS], F32, name="stat_rows")
+        for first, count in ((32, 32), (64, 64)):
+            nc.vector.memset(stat_rows[first : first + count, :], 0.0)
+        for n, saved in enumerate((rstd, mu)):
+            nc.sync.dma_start(
+                out=stat_rows[n * PASSES : (n + 1) * PASSES, :],
+                in_=saved.rearrange("b i j -> (b i j)").rearrange("(c t) -> c t", t=K_PASS),
             )
-            nc.vector.tensor_tensor(
-                out=coef[:, passes, 1, :], in0=coef[:, passes, 0, :], in1=mu_t[:, passes, :], op=ALU.mult
-            )
-
-        load_statistics(nc.sync, slice(0, HEAD_PASSES))
+        nc.sync.dma_start(out=small_rows[0:1, :FEAT], in_=gamma_e.unsqueeze(0))
         load_gradient(0)
+        nc.scalar.dma_start(out=small_rows[0:1, FEAT:], in_=node_mask.rearrange("b n -> (b n)").unsqueeze(0))
         load_gradient(1)
-        mask_all = const.tile([P, P], BF16, name="mask_all")
-        nc.scalar.dma_start(out=mask_all[:], in_=node_mask.rearrange("b n -> (b n)").partition_broadcast(P))
         node_bf = const.tile([P, FEAT], BF16, name="node_bf")
         nc.scalar.dma_start(out=node_bf[:], in_=new_node.rearrange("b n f -> (b n) f"))
-        load_statistics(nc.sync, slice(HEAD_PASSES, PASSES))
         ident = const.tile([P, P], F32, name="ident")
         make_identity(nc, ident[:])
-        build_coefficients(slice(0, HEAD_PASSES))
+        gamma_ps = psum_gx.tile([P, FEAT], F32, name="gx")
+        nc.tensor.matmul(out=gamma_ps[:], lhsT=ones[:], rhs=small_rows[:, :FEAT], start=True, stop=True)
+        stat_ps = psum_rs.tile([P, FEAT], F32, name="rs_ps")
+        for s in range(PACK):
+            nc.tensor.transpose(
+                stat_ps[:, s * P : (s + 1) * P], stat_rows[:].rearrange("r (p s) -> r s p", s=PACK)[:, s, :], ident[:]
+            )
+        stats_t = const.tile([P, 2, PASSES, PACK], F32, name="stats_t")
+        nc.vector.tensor_copy(
+            out=stats_t[:].rearrange("p n c s -> p (n c) s"),
+            in_=stat_ps[:].rearrange("p (s r) -> p r s", s=PACK)[:, : 2 * PASSES, :],
+        )
+        rstd_t, mu_t = stats_t[:, 0, :, :], stats_t[:, 1, :, :]
+        mask_all = psum_cs.tile([P, FEAT], F32, name="cs1")
+        nc.tensor.matmul(out=mask_all[:, :P], lhsT=ones[:], rhs=small_rows[:, FEAT:], start=True, stop=True)
+
+        coef = const.tile([P, PASSES, 2, PACK], F32, name="coef")
+
+        def build_coefficients():
+            nc.vector.scalar_tensor_tensor(
+                out=coef[:, :, 0, :], in0=rstd_t, scalar=-1.0 / FEAT, in1=rstd_t, op0=ALU.mult, op1=ALU.mult
+            )
+            nc.vector.tensor_tensor(out=coef[:, :, 1, :], in0=coef[:, :, 0, :], in1=mu_t, op=ALU.mult)
 
         row_sums_t = const.tile([P, FBLOCKS, P], F32, name="row_sums_t")
         col_sums_t = const.tile([P, FBLOCKS, P], F32, name="col_sums_t")
@@ -138,7 +145,7 @@ def tile_densegatlayer_pb_v_kernel(
         def pick_masks():
             nc.vector.tensor_tensor(
                 out=pick_i[:],
-                in0=mask_all[:].rearrange("p (c g) -> p c g", g=ROWS_PER_PASS),
+                in0=mask_all[:, :P].rearrange("p (c g) -> p c g", g=ROWS_PER_PASS),
                 in1=sel_row[:].unsqueeze(1).to_broadcast([P, PASSES, ROWS_PER_PASS]),
                 op=ALU.mult,
             )
@@ -172,7 +179,7 @@ def tile_densegatlayer_pb_v_kernel(
 
         def scaled_gradient(c):
             g_raw = state[("g", c)]
-            grr = work.tile([P, PACK, FEAT], F32, name="grr")
+            grr = work.tile([P, PACK, FEAT], F32, name="grr", bufs=4)
             sum_g = small.tile([P, PACK], F32, name="sum_g")
             for s in range(PACK):
                 nc.vector.scalar_tensor_tensor(
@@ -186,7 +193,7 @@ def tile_densegatlayer_pb_v_kernel(
             y_raw, grr = state[("y", c)], state[("grr", c)]
             junk = work.tile([P, PACK, FEAT], BF16, name="junk", bufs=1)
             sum_gy = small.tile([P, PACK], F32, name="sum_gy")
-            for s in range(PACK):
+            for s in reversed(range(PACK)):
                 nc.vector.scalar_tensor_tensor(
                     out=junk[:, s, :], in0=y_raw[:, s, :], scalar=mu_t[:, c, s : s + 1], in1=grr[:, s, :],
                     op0=ALU.subtract, op1=ALU.mult, accum_out=sum_gy[:, s : s + 1],
@@ -220,8 +227,15 @@ def tile_densegatlayer_pb_v_kernel(
 
         def add_line_on_gpsimd(c):
             y_raw, grr = state[("y", c)], state[("grr", c)]
-            for s in range(VEC_SLOTS, PACK):
-                nc.gpsimd.tensor_tensor(out=grr[:, s, :], in0=grr[:, s, :], in1=y_raw[:, s, :], op=ALU.add)
+            gate = small.tile([P, 1], F32, name="gate")
+            nc.gpsimd.tensor_copy(out=gate[:], in_=state[("shift", c + 1)][:, 0:1])
+            slots = slice(VEC_SLOTS, PACK)
+            nc.gpsimd.tensor_tensor(
+                out=grr[:, slots, :].rearrange("p s f -> p (s f)"),
+                in0=grr[:, slots, :].rearrange("p s f -> p (s f)"),
+                in1=y_raw[:, slots, :].rearrange("p s f -> p (s f)"),
+                op=ALU.add,
+            )
 
         def line_of_y_on_vector(c, slots):
             y_raw = state[("y", c)]
@@ -242,7 +256,7 @@ def tile_densegatlayer_pb_v_kernel(
             )
 
         def regroup_gradient(c):
-            dy_grp = work.tile([P, FEAT, PACK], BF16, name="dy_grp", align_bytes=64)
+            dy_grp = work.tile([P, FEAT, PACK], BF16, name="dy_grp", bufs=2, align_bytes=64)
             regroup(nc.scalar.copy, dy_grp, state[("grr", c)])
             state[("dy_grp", c)] = dy_grp
 
@@ -312,8 +326,8 @@ def tile_densegatlayer_pb_v_kernel(
 
         def mask_edges(c):
             e_raw = state[("e", c)]
-            xe_lin = work.tile([P, PACK, FEAT], BF16, name="xe_lin", bufs=3)
-            vec_slots = PACK if c >= PASSES - LAG else MASK_VEC_SLOTS
+            xe_lin = work.tile([P, PACK, FEAT], BF16, name="xe_lin", bufs=2)
+            vec_slots = PACK if c >= PASSES - LAG - 1 else MASK_VEC_SLOTS
             for s in range(vec_slots):
                 nc.vector.tensor_scalar(
                     out=xe_lin[:, s, :], in0=e_raw[:, s, :], scalar1=edge_mask[:, c, s : s + 1], scalar2=None, op0=ALU.mult
@@ -355,7 +369,7 @@ def tile_densegatlayer_pb_v_kernel(
                     for m, acc in enumerate(state["acc"]):
                         nc.scalar.copy(out=first_part[:, m, :], in_=acc[:])
             else:
-                missed = (FIRST_PART + 1) // 2
+                missed = (FIRST_PART + CATCH_UP_STEPS - 1) // CATCH_UP_STEPS
                 caught_up = range((c - FIRST_PART) * missed, min((c - FIRST_PART + 1) * missed, FIRST_PART))
                 for m, acc in enumerate(state["acc"]):
                     for past in caught_up:
@@ -374,6 +388,8 @@ def tile_densegatlayer_pb_v_kernel(
                 nc.vector.tensor_tensor(out=block[:], in0=acc[:], in1=add, op=ALU.add)
             nc.sync.dma_start(out=out[2 * FEAT + m * P : 2 * FEAT + (m + 1) * P, :], in_=block[:])
 
+        last = PASSES - 1
+
         def one_step(step):
             if step + 2 < PASSES:
                 load_gradient(step + 2)
@@ -383,49 +399,59 @@ def tile_densegatlayer_pb_v_kernel(
                 build_selectors()
             scaled_gradient(step)
             if step == 0:
+                build_coefficients()
                 pick_masks()
                 reduce_masks()
                 nc.scalar.copy(out=node_f32[:], in_=node_bf[:])
+            if step >= 3:
+                flush_row_sums(step - 3)
+                if step - 3 == PASSES_PER_GRAPH - 1:
+                    flush_col_sums(0)
             if step >= 1:
-                add_line_on_gpsimd(step - 1)
-                add_line_on_vector(step - 1, slice(0, VEC_SLOTS))
+                line_of_y(step - 1, SLOT_ORDER)
+            if step >= 2:
+                add_line_on_gpsimd(step - 2)
+                add_line_on_vector(step - 2, slice(0, VEC_SLOTS))
+                transpose_for_col_sums(step - 2)
+                transpose_for_row_sums(step - 2)
+            if step >= LAG:
+                mask_edges(step - LAG)
+            if step == last:
+                quantise_edges(step - LAG - 1)
+                quantise_gradient(step - 3)
+                add_line_on_vector(step - 1, slice(0, PACK))
+                flush_row_sums(step - 2)
             gradient_dot_y(step)
             if step == 0:
                 multiply_masks()
-            if step == 1:
-                build_coefficients(slice(HEAD_PASSES, PASSES))
-            if step >= LAG:
-                mask_edges(step - LAG)
+            if LAG + 1 <= step < last:
+                quantise_edges(step - LAG - 1)
             line_slope(step)
             if step >= 2:
-                flush_row_sums(step - 2)
-                if step - 2 == PASSES_PER_GRAPH - 1:
-                    flush_col_sums(0)
-            line_shift(step)
-            line_of_y(step, SLOT_ORDER if step < PASSES - 1 else SLOT_ORDER[VEC_SLOTS:])
-            if step >= 1:
-                regroup_gradient(step - 1)
-                transpose_for_col_sums(step - 1)
-                if step == PASSES - 1:
-                    state["late"] = psum_gx.tile([P, FEAT], F32, name="gx")
-                    multiply_late(state["late"], 0, range(FIRST_PART, step - LAG - 1))
-                transpose_for_row_sums(step - 1)
-            if step == PASSES - 1:
-                line_of_y_on_vector(step, SLOT_ORDER[:VEC_SLOTS])
-                flush_row_sums(step - 1)
-                add_line_on_vector(step, slice(VEC_SLOTS, PACK))
-                add_line_on_vector(step, slice(0, VEC_SLOTS))
-            if step >= 2:
+                regroup_gradient(step - 2)
+            if step == last:
                 quantise_gradient(step - 2)
-            if step >= LAG + 1:
-                quantise_edges(step - LAG - 1)
-                if step < PASSES - 1:
-                    multiply_edges(step - LAG - 1)
+            elif step >= 3:
+                quantise_gradient(step - 3)
+            line_shift(step)
+            if step == last:
+                regroup_gradient(step - 1)
+                line_of_y(step, SLOT_ORDER[VEC_SLOTS:])
+                transpose_for_col_sums(step - 1)
+                transpose_for_row_sums(step - 1)
+                multiply_edges(step - LAG - 1)
+                state["late"] = psum_gx.tile([P, FEAT], F32, name="gx")
+                multiply_late(state["late"], 0, range(FIRST_PART, step - LAG))
+                line_of_y_on_vector(step, SLOT_ORDER[:VEC_SLOTS])
+                add_line_on_vector(step, slice(VEC_SLOTS, PACK))
+                flush_row_sums(step - 1)
+                add_line_on_vector(step, slice(0, VEC_SLOTS))
+            elif step >= LAG + 1:
+                multiply_edges(step - LAG - 1)
             if step >= LAG:
                 regroup_edges(step - LAG, nc.scalar.copy)
 
         def last_steps():
-            last = PASSES - 1
             load_edges(last)
             transpose_for_row_sums(last)
             transpose_for_col_sums(last)
@@ -436,15 +462,12 @@ def tile_densegatlayer_pb_v_kernel(
             row_sums = turn_sums(row_sums_t, psum_rs.tile([P, FEAT], F32, name="rs_ps"))
             quantise_edges(last - 3)
             late0_ps = state["late"]
-            multiply_edges(last - 4)
-            multiply_late(late0_ps, 0, range(last - 4, last - 3))
             multiply_edges(last - 3)
             flush_col_sums(1)
             regroup_edges(last - 2, nc.vector.tensor_copy)
             node_product(0, 0, row_sums, psum_cs.tile([P, FEAT], F32, name="cs1"))
             node_product(0, 1, row_sums, psum_cs.tile([P, FEAT], F32, name="cs2"))
             mask_edges(last - 1)
-            quantise_gradient(last)
             quantise_edges(last - 2)
             col_sums = turn_sums(col_sums_t, psum_cs.tile([P, FEAT], F32, name="cs0"))
             node_product(0, 2, row_sums, psum_cs.tile([P, FEAT], F32, name="cs1"))
@@ -457,6 +480,7 @@ def tile_densegatlayer_pb_v_kernel(
             mask_edges(last)
             quantise_edges(last - 1)
             regroup_edges(last, nc.vector.tensor_copy)
+            quantise_gradient(last)
             node_product(FEAT, 0, col_sums, psum_cs.tile([P, FEAT], F32, name="cs1"))
             node_product(FEAT, 1, col_sums, psum_cs.tile([P, FEAT], F32, name="cs2"))
             multiply_edges(last - 1)

@@ -26,12 +26,12 @@ ROWS_PER_PASS = K_PASS // NODES
 PARTS_PER_ROW = P // ROWS_PER_PASS
 FBLOCKS = FEAT // P
 LIVE_TILES = 2
-FIRST_PART = 10
+FIRST_PART = 11
 CATCH_UP_STEPS = 2
 SLOT_ORDER = (2, 3, 0, 1)
 MASK_VEC_SLOTS = 2
 VEC_SLOTS = 2
-LAG = 3
+LAG = 2
 
 FLOPS = 2 * TOKENS * FEAT * FEAT + 2 * 2 * GRAPHS * NODES * FEAT * FEAT
 
@@ -93,6 +93,10 @@ def tile_densegatlayer_pb_v_kernel(
         nc.scalar.dma_start(out=node_bf[:], in_=new_node.rearrange("b n f -> (b n) f"))
         ident = const.tile([P, P], F32, name="ident")
         make_identity(nc, ident[:])
+        swap = const.tile([P, P], F32, name="swap")
+        halves = [m[:].rearrange("p (i h q) -> p h i q", h=2, q=PARTS_PER_ROW // 2) for m in (swap, ident)]
+        for h in range(2):
+            nc.vector.tensor_copy(out=halves[0][:, h, :, :], in_=halves[1][:, 1 - h, :, :])
         gamma_ps = psum_gx.tile([P, FEAT], F32, name="gx")
         nc.tensor.matmul(out=gamma_ps[:], lhsT=ones[:], rhs=small_rows[:, :FEAT], start=True, stop=True)
         stat_ps = psum_rs.tile([P, FEAT], F32, name="rs_ps")
@@ -260,16 +264,18 @@ def tile_densegatlayer_pb_v_kernel(
             regroup(nc.scalar.copy, dy_grp, state[("grr", c)])
             state[("dy_grp", c)] = dy_grp
 
+        def row_turns(c):
+            return (ident, swap) if c < PASSES - 1 else (ident,)
+
         def transpose_for_row_sums(c):
             dy = state[("grr", c)]
             rs_ps = psum_rs.tile([P, FEAT], F32, name="rs_ps")
-            for n, s in enumerate(SLOT_ORDER):
-                for k in range(FBLOCKS):
-                    nc.tensor.matmul(
-                        out=rs_ps[:, k * P : (k + 1) * P], lhsT=dy[:, s, k * P : (k + 1) * P], rhs=ident[:],
-                        is_transpose=True,
-                        start=(n == 0 and k == 0), stop=(n == PACK - 1 and k == FBLOCKS - 1),
-                    )
+            turns = [(s, k, order) for s in SLOT_ORDER for k in range(FBLOCKS) for order in row_turns(c)]
+            for n, (s, k, order) in enumerate(turns):
+                nc.tensor.matmul(
+                    out=rs_ps[:, k * P : (k + 1) * P], lhsT=dy[:, s, k * P : (k + 1) * P], rhs=order[:],
+                    is_transpose=True, start=(n == 0), stop=(n == len(turns) - 1),
+                )
             state[("rs", c)] = rs_ps
 
         def transpose_for_col_sums(c):
@@ -298,7 +304,9 @@ def tile_densegatlayer_pb_v_kernel(
         def flush_row_sums(c):
             nc.vector.tensor_reduce(
                 out=row_sums_t[:, :, c * ROWS_PER_PASS : (c + 1) * ROWS_PER_PASS],
-                in_=state[("rs", c)][:].rearrange("p (k i q) -> p k i q", k=FBLOCKS, q=PARTS_PER_ROW),
+                in_=state[("rs", c)][:].rearrange("p (k i q) -> p k i q", k=FBLOCKS, q=PARTS_PER_ROW)[
+                    :, :, :, : PARTS_PER_ROW // len(row_turns(c))
+                ],
                 axis=AX.X, op=ALU.add,
             )
 
@@ -380,13 +388,14 @@ def tile_densegatlayer_pb_v_kernel(
             for c in passes:
                 edge_pass(acc, m, c, c == FIRST_PART, c == PASSES - 1)
 
-        def store_edge_block(m, acc, add=None):
-            block = tail.tile([P, FEAT], F32, name="prod", bufs=6)
-            if add is None:
-                nc.vector.tensor_copy(out=block[:], in_=acc[:])
+        def store_edge_block(m, acc):
+            if m < LIVE_TILES:
+                block = first_part[:, m, :]
+                nc.vector.tensor_tensor(out=block, in0=acc[:], in1=block, op=ALU.add)
             else:
-                nc.vector.tensor_tensor(out=block[:], in0=acc[:], in1=add, op=ALU.add)
-            nc.sync.dma_start(out=out[2 * FEAT + m * P : 2 * FEAT + (m + 1) * P, :], in_=block[:])
+                block = tail.tile([P, FEAT], F32, name="prod", bufs=6)[:]
+                nc.vector.tensor_copy(out=block, in_=acc[:])
+            nc.sync.dma_start(out=out[2 * FEAT + m * P : 2 * FEAT + (m + 1) * P, :], in_=block)
 
         last = PASSES - 1
 
@@ -397,18 +406,18 @@ def tile_densegatlayer_pb_v_kernel(
                 load_edges(step + 2 - LAG)
             if step == 0:
                 build_selectors()
+                pick_masks()
+                reduce_masks()
             scaled_gradient(step)
             if step == 0:
                 build_coefficients()
-                pick_masks()
-                reduce_masks()
                 nc.scalar.copy(out=node_f32[:], in_=node_bf[:])
             if step >= 3:
                 flush_row_sums(step - 3)
                 if step - 3 == PASSES_PER_GRAPH - 1:
                     flush_col_sums(0)
             if step >= 1:
-                line_of_y(step - 1, SLOT_ORDER)
+                line_of_y(step - 1, SLOT_ORDER if step < last else SLOT_ORDER[VEC_SLOTS:])
             if step >= 2:
                 add_line_on_gpsimd(step - 2)
                 add_line_on_vector(step - 2, slice(0, VEC_SLOTS))
@@ -419,7 +428,9 @@ def tile_densegatlayer_pb_v_kernel(
             if step == last:
                 quantise_edges(step - LAG - 1)
                 quantise_gradient(step - 3)
-                add_line_on_vector(step - 1, slice(0, PACK))
+                line_of_y_on_vector(step - 1, SLOT_ORDER[:VEC_SLOTS])
+                add_line_on_vector(step - 1, slice(VEC_SLOTS, PACK))
+                add_line_on_vector(step - 1, slice(0, VEC_SLOTS))
                 flush_row_sums(step - 2)
             gradient_dot_y(step)
             if step == 0:
@@ -452,47 +463,40 @@ def tile_densegatlayer_pb_v_kernel(
                 regroup_edges(step - LAG, nc.scalar.copy)
 
         def last_steps():
-            load_edges(last)
             transpose_for_row_sums(last)
             transpose_for_col_sums(last)
             regroup_gradient(last)
-            mask_edges(last - 2)
+            mask_edges(last - 1)
             quantise_gradient(last - 1)
+            quantise_edges(last - 2)
             flush_row_sums(last)
             row_sums = turn_sums(row_sums_t, psum_rs.tile([P, FEAT], F32, name="rs_ps"))
-            quantise_edges(last - 3)
             late0_ps = state["late"]
-            multiply_edges(last - 3)
+            multiply_edges(last - 2)
             flush_col_sums(1)
-            regroup_edges(last - 2, nc.vector.tensor_copy)
+            regroup_edges(last - 1, nc.vector.tensor_copy)
             node_product(0, 0, row_sums, psum_cs.tile([P, FEAT], F32, name="cs1"))
             node_product(0, 1, row_sums, psum_cs.tile([P, FEAT], F32, name="cs2"))
-            mask_edges(last - 1)
-            quantise_edges(last - 2)
-            col_sums = turn_sums(col_sums_t, psum_cs.tile([P, FEAT], F32, name="cs0"))
-            node_product(0, 2, row_sums, psum_cs.tile([P, FEAT], F32, name="cs1"))
-            node_product(0, 3, row_sums, psum_cs.tile([P, FEAT], F32, name="cs2"))
-            multiply_edges(last - 2)
-            late1_ps = psum_rs.tile([P, FEAT], F32, name="rs_ps")
-            multiply_late(late1_ps, 1, range(FIRST_PART, last - 1))
-            multiply_late(late0_ps, 0, range(last - 3, last - 1))
-            regroup_edges(last - 1, nc.vector.tensor_copy)
             mask_edges(last)
             quantise_edges(last - 1)
+            col_sums = turn_sums(col_sums_t, psum_cs.tile([P, FEAT], F32, name="cs0"))
+            node_product(0, 2, row_sums, psum_cs.tile([P, FEAT], F32, name="cs3"))
+            node_product(0, 3, row_sums, psum_cs.tile([P, FEAT], F32, name="cs1"))
+            multiply_edges(last - 1)
+            late1_ps = psum_rs.tile([P, FEAT], F32, name="rs_ps")
+            multiply_late(late1_ps, 1, range(FIRST_PART, last))
+            multiply_late(late0_ps, 0, range(last - 2, last))
             regroup_edges(last, nc.vector.tensor_copy)
             quantise_gradient(last)
-            node_product(FEAT, 0, col_sums, psum_cs.tile([P, FEAT], F32, name="cs1"))
-            node_product(FEAT, 1, col_sums, psum_cs.tile([P, FEAT], F32, name="cs2"))
-            multiply_edges(last - 1)
             quantise_edges(last)
-            node_product(FEAT, 2, col_sums, psum_cs.tile([P, FEAT], F32, name="cs1"))
+            node_product(FEAT, 0, col_sums, psum_cs.tile([P, FEAT], F32, name="cs2"))
             multiply_edges(last)
-            for m, acc in enumerate(state["acc"]):
-                store_edge_block(LIVE_TILES + m, acc)
-            node_product(FEAT, 3, col_sums, psum_cs.tile([P, FEAT], F32, name="cs2"))
             for m, acc in enumerate((late0_ps, late1_ps)):
-                multiply_late(acc, m, range(last - 1, PASSES))
-                store_edge_block(m, acc, first_part[:, m, :])
+                multiply_late(acc, m, range(last, PASSES))
+            for m, acc in enumerate((*state["acc"], late0_ps, late1_ps)):
+                store_edge_block((LIVE_TILES + m) % FBLOCKS, acc)
+            for m in range(1, FBLOCKS):
+                node_product(FEAT, m, col_sums, psum_cs.tile([P, FEAT], F32, name="cs%d" % (m % 3 + 1)))
 
         with tc.manual_schedule(
             engines={mybir.EngineType.PE, mybir.EngineType.Activation, mybir.EngineType.DVE, mybir.EngineType.Pool}

@@ -220,6 +220,20 @@ def tile_densegatlayer_pb_v_kernel(
             )
             state[("shift", c)] = shift
 
+        def half_shift_on_gpsimd(c):
+            mean_g = small.tile([P, PACK], F32, name="mean_g")
+            nc.gpsimd.tensor_scalar(
+                out=mean_g[:], in0=state[("sum_g", c)][:], scalar1=-1.0 / FEAT, scalar2=0.0, op0=ALU.mult, op1=ALU.add
+            )
+            state[("mean_g", c)] = mean_g
+
+        def line_shift_on_gpsimd(c):
+            shift = small.tile([P, PACK], F32, name="shift")
+            nc.gpsimd.tensor_tensor(
+                out=shift[:], in0=state[("mean_g", c)][:], in1=state[("line", c)][:, 1, :], op=ALU.subtract
+            )
+            state[("shift", c)] = shift
+
         def line_of_y(c, slots):
             y_raw = state[("y", c)]
             line, shift = state[("line", c)], state[("shift", c)]
@@ -231,8 +245,6 @@ def tile_densegatlayer_pb_v_kernel(
 
         def add_line_on_gpsimd(c):
             y_raw, grr = state[("y", c)], state[("grr", c)]
-            gate = small.tile([P, 1], F32, name="gate")
-            nc.gpsimd.tensor_copy(out=gate[:], in_=state[("shift", c + 1)][:, 0:1])
             slots = slice(VEC_SLOTS, PACK)
             nc.gpsimd.tensor_tensor(
                 out=grr[:, slots, :].rearrange("p s f -> p (s f)"),
@@ -423,6 +435,8 @@ def tile_densegatlayer_pb_v_kernel(
                 add_line_on_vector(step - 2, slice(0, VEC_SLOTS))
                 transpose_for_col_sums(step - 2)
                 transpose_for_row_sums(step - 2)
+            if step < last:
+                half_shift_on_gpsimd(step)
             if step >= LAG:
                 mask_edges(step - LAG)
             if step == last:
@@ -438,14 +452,16 @@ def tile_densegatlayer_pb_v_kernel(
             if LAG + 1 <= step < last:
                 quantise_edges(step - LAG - 1)
             line_slope(step)
+            if step < last:
+                line_shift_on_gpsimd(step)
             if step >= 2:
                 regroup_gradient(step - 2)
             if step == last:
                 quantise_gradient(step - 2)
             elif step >= 3:
                 quantise_gradient(step - 3)
-            line_shift(step)
             if step == last:
+                line_shift(step)
                 regroup_gradient(step - 1)
                 line_of_y(step, SLOT_ORDER[VEC_SLOTS:])
                 transpose_for_col_sums(step - 1)

from contextlib import ExitStack

import concourse.mybir as mybir
from concourse.masks import make_identity

F32 = mybir.dt.float32
BF16 = mybir.dt.bfloat16
U32 = mybir.dt.uint32
U8 = mybir.dt.uint8
E4M3_X4 = mybir.dt.float8_e4m3fn_x4
E5M2_X4 = mybir.dt.float8_e5m2_x4
ALU = mybir.AluOpType
ACT = mybir.ActivationFunctionType
AX = mybir.AxisListType

P = 128
PACK = 4
GRAPHS = 2
NODES = 64
FEAT = 512
TOKENS = GRAPHS * NODES * NODES
K_PASS = P * PACK
PASSES = TOKENS // K_PASS
PASSES_PER_GRAPH = PASSES // GRAPHS
ROWS_PER_PASS = K_PASS // NODES
PARTS_PER_ROW = P // ROWS_PER_PASS
FBLOCKS = FEAT // P
LIVE_TILES = 2
FIRST_PART = 11
CATCH_UP_STEPS = 2
SLOT_ORDER = (2, 3, 0, 1)
MASK_VEC_SLOTS = 2
VEC_SLOTS = 2
LAG = 2

FLOPS = 2 * TOKENS * FEAT * FEAT + 2 * 2 * GRAPHS * NODES * FEAT * FEAT


def tile_densegatlayer_pb_v_kernel(
    tc, new_node, emb_edge, node_mask, Wedge, bedge, gamma_e, beta_e, y, mu, rstd, grad_out, out
):
    nc = tc.nc
    emb_rows = emb_edge.rearrange("b i j f -> (b i j) f")
    grad_rows = grad_out.rearrange("b i j f -> (b i j) f")
    y_rows = y.rearrange("b i j f -> (b i j) f")

    with ExitStack() as ctx:
        const = ctx.enter_context(tc.tile_pool(name="const", bufs=1))
        loads = ctx.enter_context(tc.tile_pool(name="loads", bufs=3))
        work = ctx.enter_context(tc.tile_pool(name="work", bufs=3))
        small = ctx.enter_context(tc.tile_pool(name="small", bufs=4))
        tail = ctx.enter_context(tc.tile_pool(name="tail", bufs=1))
        psum_cs = ctx.enter_context(tc.psum_pool(name="psum_cs", bufs=1))
        psum_rs = ctx.enter_context(tc.psum_pool(name="psum_rs", bufs=1))
        psum_mx = ctx.enter_context(tc.psum_pool(name="psum_mx", bufs=1))
        psum_gx = ctx.enter_context(tc.psum_pool(name="psum_gx", bufs=1))

        state = {}

        def pass_rows(rows_of, c):
            return rows_of[c * K_PASS : (c + 1) * K_PASS, :].rearrange("(p s) f -> p s f", s=PACK)

        def load_gradient(c):
            g_raw = loads.tile([P, PACK, FEAT], BF16, name="g_raw")
            nc.sync.dma_start(out=g_raw[:], in_=pass_rows(grad_rows, c))
            y_raw = loads.tile([P, PACK, FEAT], F32, name="y_raw", bufs=5)
            nc.sync.dma_start(out=y_raw[:], in_=pass_rows(y_rows, c))
            state[("g", c)] = g_raw
            state[("y", c)] = y_raw

        def load_edges(c):
            e_raw = loads.tile([P, PACK, FEAT], BF16, name="e_raw")
            nc.sync.dma_start(out=e_raw[:], in_=pass_rows(emb_rows, c))
            state[("e", c)] = e_raw

        ones = const.tile([P, P], BF16, name="ones")
        nc.vector.memset(ones[:], 1.0)
        small_rows = const.tile([P, FEAT + P], BF16, name="small_rows")
        nc.vector.memset(small_rows[:], 0.0)
        stat_rows = const.tile([P, K_PASS], F32, name="stat_rows")
        for first, count in ((32, 32), (64, 64)):
            nc.vector.memset(stat_rows[first : first + count, :], 0.0)
        for n, saved in enumerate((rstd, mu)):
            nc.sync.dma_start(
                out=stat_rows[n * PASSES : (n + 1) * PASSES, :],
                in_=saved.rearrange("b i j -> (b i j)").rearrange("(c t) -> c t", t=K_PASS),
            )
        nc.sync.dma_start(out=small_rows[0:1, :FEAT], in_=gamma_e.unsqueeze(0))
        load_gradient(0)
        nc.scalar.dma_start(out=small_rows[0:1, FEAT:], in_=node_mask.rearrange("b n -> (b n)").unsqueeze(0))
        load_gradient(1)
        node_bf = const.tile([P, FEAT], BF16, name="node_bf")
        nc.scalar.dma_start(out=node_bf[:], in_=new_node.rearrange("b n f -> (b n) f"))
        ident = const.tile([P, P], F32, name="ident")
        make_identity(nc, ident[:])
        swap = const.tile([P, P], F32, name="swap")
        halves = [m[:].rearrange("p (i h q) -> p h i q", h=2, q=PARTS_PER_ROW // 2) for m in (swap, ident)]
        for h in range(2):
            nc.vector.tensor_copy(out=halves[0][:, h, :, :], in_=halves[1][:, 1 - h, :, :])
        gamma_ps = psum_gx.tile([P, FEAT], F32, name="gx")
        nc.tensor.matmul(out=gamma_ps[:], lhsT=ones[:], rhs=small_rows[:, :FEAT], start=True, stop=True)
        stat_ps = psum_rs.tile([P, FEAT], F32, name="rs_ps")
        for s in range(PACK):
            nc.tensor.transpose(
                stat_ps[:, s * P : (s + 1) * P], stat_rows[:].rearrange("r (p s) -> r s p", s=PACK)[:, s, :], ident[:]
            )
        stats_t = const.tile([P, 2, PASSES, PACK], F32, name="stats_t")
        nc.vector.tensor_copy(
            out=stats_t[:].rearrange("p n c s -> p (n c) s"),
            in_=stat_ps[:].rearrange("p (s r) -> p r s", s=PACK)[:, : 2 * PASSES, :],
        )
        rstd_t, mu_t = stats_t[:, 0, :, :], stats_t[:, 1, :, :]
        mask_all = psum_cs.tile([P, FEAT], F32, name="cs1")
        nc.tensor.matmul(out=mask_all[:, :P], lhsT=ones[:], rhs=small_rows[:, FEAT:], start=True, stop=True)

        coef = const.tile([P, PASSES, 2, PACK], F32, name="coef")

        def build_coefficients():
            nc.vector.scalar_tensor_tensor(
                out=coef[:, :, 0, :], in0=rstd_t, scalar=-1.0 / FEAT, in1=rstd_t, op0=ALU.mult, op1=ALU.mult
            )
            nc.vector.tensor_tensor(out=coef[:, :, 1, :], in0=coef[:, :, 0, :], in1=mu_t, op=ALU.mult)

        row_sums_t = const.tile([P, FBLOCKS, P], F32, name="row_sums_t")
        col_sums_t = const.tile([P, FBLOCKS, P], F32, name="col_sums_t")
        x_codes = const.tile([P, PASSES, FEAT], U32, name="x_codes", align_bytes=64)
        x_scales = const.tile([P, PASSES, FEAT], U8, name="x_scales", align_bytes=64)
        d_codes = const.tile([P, PASSES, FEAT], U32, name="d_codes", align_bytes=64)
        d_scales = const.tile([P, PASSES, FEAT], U8, name="d_scales", align_bytes=64)
        edge_mask = const.tile([P, PASSES, PACK], F32, name="edge_mask")
        node_f32 = const.tile([P, FEAT], F32, name="node_f32")
        first_part = const.tile([P, LIVE_TILES, FEAT], F32, name="first_part")

        sel_row = const.tile([P, ROWS_PER_PASS], F32, name="sel_row")
        sel_col = const.tile([P, PARTS_PER_ROW], F32, name="sel_col")
        pick_i = const.tile([P, PASSES, ROWS_PER_PASS], F32, name="pick_i")
        pick_j = const.tile([P, GRAPHS * PACK, PARTS_PER_ROW], F32, name="pick_j")
        mask_i = const.tile([P, PASSES], F32, name="mask_i")
        mask_j = const.tile([P, GRAPHS * PACK], F32, name="mask_j")

        def build_selectors():
            nc.vector.tensor_reduce(
                out=sel_row[:], in_=ident[:].rearrange("p (g q) -> p g q", q=PARTS_PER_ROW), axis=AX.X, op=ALU.add
            )
            nc.vector.tensor_reduce(
                out=sel_col[:], in_=ident[:].rearrange("p (g q) -> p q g", q=PARTS_PER_ROW), axis=AX.X, op=ALU.add
            )

        def pick_masks():
            nc.vector.tensor_tensor(
                out=pick_i[:],
                in0=mask_all[:, :P].rearrange("p (c g) -> p c g", g=ROWS_PER_PASS),
                in1=sel_row[:].unsqueeze(1).to_broadcast([P, PASSES, ROWS_PER_PASS]),
                op=ALU.mult,
            )
            for b in range(GRAPHS):
                nc.vector.tensor_tensor(
                    out=pick_j[:, b * PACK : (b + 1) * PACK, :],
                    in0=mask_all[:, b * NODES : (b + 1) * NODES].rearrange("p (q s) -> p s q", s=PACK),
                    in1=sel_col[:].unsqueeze(1).to_broadcast([P, PACK, PARTS_PER_ROW]),
                    op=ALU.mult,
                )

        def reduce_masks():
            nc.vector.tensor_reduce(out=mask_i[:], in_=pick_i[:], axis=AX.X, op=ALU.add)
            nc.vector.tensor_reduce(out=mask_j[:], in_=pick_j[:], axis=AX.X, op=ALU.add)

        def multiply_masks():
            for b in range(GRAPHS):
                graph_passes = slice(b * PASSES_PER_GRAPH, (b + 1) * PASSES_PER_GRAPH)
                nc.vector.tensor_tensor(
                    out=edge_mask[:, graph_passes, :],
                    in0=mask_i[:, graph_passes].unsqueeze(2).to_broadcast([P, PASSES_PER_GRAPH, PACK]),
                    in1=mask_j[:, b * PACK : (b + 1) * PACK].unsqueeze(1).to_broadcast([P, PASSES_PER_GRAPH, PACK]),
                    op=ALU.mult,
                )

        def regroup(copy, dst, src):
            copy(
                out=dst[:].rearrange("p (c i) s -> p c s i", i=4),
                in_=src[:].rearrange("p s (c i) -> p c s i", i=4),
            )

        def scaled_gradient(c):
            g_raw = state[("g", c)]
            grr = work.tile([P, PACK, FEAT], F32, name="grr", bufs=4)
            sum_g = small.tile([P, PACK], F32, name="sum_g")
            for s in range(PACK):
                nc.vector.scalar_tensor_tensor(
                    out=grr[:, s, :], in0=g_raw[:, s, :], scalar=rstd_t[:, c, s : s + 1], in1=gamma_ps[:],
                    op0=ALU.mult, op1=ALU.mult, accum_out=sum_g[:, s : s + 1],
                )
            state[("grr", c)] = grr
            state[("sum_g", c)] = sum_g

        def gradient_dot_y(c):
            y_raw, grr = state[("y", c)], state[("grr", c)]
            junk = work.tile([P, PACK, FEAT], BF16, name="junk", bufs=1)
            sum_gy = small.tile([P, PACK], F32, name="sum_gy")
            for s in reversed(range(PACK)):
                nc.vector.scalar_tensor_tensor(
                    out=junk[:, s, :], in0=y_raw[:, s, :], scalar=mu_t[:, c, s : s + 1], in1=grr[:, s, :],
                    op0=ALU.subtract, op1=ALU.mult, accum_out=sum_gy[:, s : s + 1],
                )
            state[("sum_gy", c)] = sum_gy

        def line_slope(c):
            sum_gy = state[("sum_gy", c)]
            line = small.tile([P, 2, PACK], F32, name="line")
            nc.vector.tensor_tensor(
                out=line[:], in0=coef[:, c, :, :], in1=sum_gy[:].unsqueeze(1).to_broadcast([P, 2, PACK]), op=ALU.mult
            )
            state[("line", c)] = line

        def line_shift(c):
            sum_g, line = state[("sum_g", c)], state[("line", c)]
            shift = small.tile([P, PACK], F32, name="shift")
            nc.vector.scalar_tensor_tensor(
                out=shift[:], in0=sum_g[:], scalar=-1.0 / FEAT, in1=line[:, 1, :], op0=ALU.mult, op1=ALU.subtract
            )
            state[("shift", c)] = shift

        def half_shift_on_gpsimd(c):
            mean_g = small.tile([P, PACK], F32, name="mean_g")
            nc.gpsimd.tensor_scalar(
                out=mean_g[:], in0=state[("sum_g", c)][:], scalar1=-1.0 / FEAT, scalar2=0.0, op0=ALU.mult, op1=ALU.add
            )
            state[("mean_g", c)] = mean_g

        def line_shift_on_gpsimd(c):
            shift = small.tile([P, PACK], F32, name="shift")
            nc.gpsimd.tensor_tensor(
                out=shift[:], in0=state[("mean_g", c)][:], in1=state[("line", c)][:, 1, :], op=ALU.subtract
            )
            state[("shift", c)] = shift

        def line_of_y(c, slots):
            y_raw = state[("y", c)]
            line, shift = state[("line", c)], state[("shift", c)]
            for s in slots:
                nc.scalar.activation(
                    out=y_raw[:, s, :], in_=y_raw[:, s, :], func=ACT.Identity,
                    scale=line[:, 0, s : s + 1], bias=shift[:, s : s + 1],
                )

        def add_line_on_gpsimd(c):
            y_raw, grr = state[("y", c)], state[("grr", c)]
            slots = slice(VEC_SLOTS, PACK)
            nc.gpsimd.tensor_tensor(
                out=grr[:, slots, :].rearrange("p s f -> p (s f)"),
                in0=grr[:, slots, :].rearrange("p s f -> p (s f)"),
                in1=y_raw[:, slots, :].rearrange("p s f -> p (s f)"),
                op=ALU.add,
            )

        def line_of_y_on_vector(c, slots):
            y_raw = state[("y", c)]
            line, shift = state[("line", c)], state[("shift", c)]
            for s in slots:
                nc.vector.tensor_scalar(
                    out=y_raw[:, s, :], in0=y_raw[:, s, :],
                    scalar1=line[:, 0, s : s + 1], scalar2=shift[:, s : s + 1], op0=ALU.mult, op1=ALU.add,
                )

        def add_line_on_vector(c, slots):
            y_raw, grr = state[("y", c)], state[("grr", c)]
            nc.vector.tensor_tensor(
                out=grr[:, slots, :].rearrange("p s f -> p (s f)"),
                in0=grr[:, slots, :].rearrange("p s f -> p (s f)"),
                in1=y_raw[:, slots, :].rearrange("p s f -> p (s f)"),
                op=ALU.add,
            )

        def regroup_gradient(c):
            dy_grp = work.tile([P, FEAT, PACK], BF16, name="dy_grp", bufs=2, align_bytes=64)
            regroup(nc.scalar.copy, dy_grp, state[("grr", c)])
            state[("dy_grp", c)] = dy_grp

        def row_turns(c):
            return (ident, swap) if c < PASSES - 1 else (ident,)

        def transpose_for_row_sums(c):
            dy = state[("grr", c)]
            rs_ps = psum_rs.tile([P, FEAT], F32, name="rs_ps")
            turns = [(s, k, order) for s in SLOT_ORDER for k in range(FBLOCKS) for order in row_turns(c)]
            for n, (s, k, order) in enumerate(turns):
                nc.tensor.matmul(
                    out=rs_ps[:, k * P : (k + 1) * P], lhsT=dy[:, s, k * P : (k + 1) * P], rhs=order[:],
                    is_transpose=True, start=(n == 0), stop=(n == len(turns) - 1),
                )
            state[("rs", c)] = rs_ps

        def transpose_for_col_sums(c):
            dy = state[("grr", c)]
            b = c // PASSES_PER_GRAPH
            first_of_graph = c % PASSES_PER_GRAPH == 0
            last_of_graph = c % PASSES_PER_GRAPH == PASSES_PER_GRAPH - 1
            if first_of_graph:
                for s in range(PACK):
                    state[("cs", b, s)] = psum_cs.tile([P, FEAT], F32, name="cs%d" % s)
            for s in SLOT_ORDER:
                cs_ps = state[("cs", b, s)]
                for k in range(FBLOCKS):
                    nc.tensor.matmul(
                        out=cs_ps[:, k * P : (k + 1) * P], lhsT=dy[:, s, k * P : (k + 1) * P], rhs=ident[:],
                        is_transpose=True,
                        start=(first_of_graph and k == 0), stop=(last_of_graph and k == FBLOCKS - 1),
                    )

        def quantise_gradient(c):
            nc.vector.quantize_mx(
                out=d_codes[:, c, :].bitcast(E5M2_X4), scales=d_scales[:, c, :],
                in_=state[("dy_grp", c)][:].rearrange("p f s -> p (f s)"),
            )

        def flush_row_sums(c):
            nc.vector.tensor_reduce(
                out=row_sums_t[:, :, c * ROWS_PER_PASS : (c + 1) * ROWS_PER_PASS],
                in_=state[("rs", c)][:].rearrange("p (k i q) -> p k i q", k=FBLOCKS, q=PARTS_PER_ROW)[
                    :, :, :, : PARTS_PER_ROW // len(row_turns(c))
                ],
                axis=AX.X, op=ALU.add,
            )

        def flush_col_sums(b):
            graph_cols = col_sums_t[:, :, b * NODES : (b + 1) * NODES].rearrange("p k (q s) -> p k q s", s=PACK)
            for s in range(PACK):
                nc.vector.tensor_reduce(
                    out=graph_cols[:, :, :, s],
                    in_=state[("cs", b, s)][:].rearrange("p (k i q) -> p k q i", k=FBLOCKS, q=PARTS_PER_ROW),
                    axis=AX.X, op=ALU.add,
                )

        def turn_sums(sums_t, back_ps):
            for k in range(FBLOCKS):
                nc.tensor.transpose(back_ps[:, k * P : (k + 1) * P], sums_t[:, k, :], ident[:])
            sums = tail.tile([P, FEAT], F32, name="sums", bufs=2)
            nc.scalar.copy(out=sums[:], in_=back_ps[:])
            return sums

        def node_product(first_row, m, sums, prod_ps):
            nc.tensor.matmul(out=prod_ps[:], lhsT=node_f32[:, m * P : (m + 1) * P], rhs=sums[:], start=True, stop=True)
            prod = tail.tile([P, FEAT], F32, name="prod", bufs=6)
            nc.scalar.copy(out=prod[:], in_=prod_ps[:])
            nc.sync.dma_start(out=out[first_row + m * P : first_row + (m + 1) * P, :], in_=prod[:])

        def mask_edges(c):
            e_raw = state[("e", c)]
            xe_lin = work.tile([P, PACK, FEAT], BF16, name="xe_lin", bufs=2)
            vec_slots = PACK if c >= PASSES - LAG - 1 else MASK_VEC_SLOTS
            for s in range(vec_slots):
                nc.vector.tensor_scalar(
                    out=xe_lin[:, s, :], in0=e_raw[:, s, :], scalar1=edge_mask[:, c, s : s + 1], scalar2=None, op0=ALU.mult
                )
            for s in range(vec_slots, PACK):
                nc.scalar.activation(
                    out=xe_lin[:, s, :], in_=e_raw[:, s, :], func=ACT.Copy, scale=edge_mask[:, c, s : s + 1]
                )
            state[("xe", c)] = xe_lin

        def regroup_edges(c, copy):
            xe_lin = state[("xe", c)]
            xe_grp = work.tile([P, FEAT, PACK], BF16, name="xe_grp", bufs=2, align_bytes=64)
            regroup(copy, xe_grp, xe_lin)
            state[("xe_grp", c)] = xe_grp

        def edge_pass(acc, m, c, first, last):
            m_cols = slice(m * P, (m + 1) * P)
            nc.tensor.matmul_mx(
                out=acc[:],
                lhsT=x_codes[:, c, m_cols].bitcast(E4M3_X4), lhsT_scale=x_scales[:, c, m_cols],
                rhs=d_codes[:, c, :].bitcast(E5M2_X4), rhs_scale=d_scales[:, c, :],
                start=first, stop=last,
            )

        def quantise_edges(c):
            nc.vector.quantize_mx(
                out=x_codes[:, c, :].bitcast(E4M3_X4), scales=x_scales[:, c, :],
                in_=state[("xe_grp", c)][:].rearrange("p f s -> p (f s)"),
            )

        def multiply_edges(c):
            if c == 0 or c == FIRST_PART:
                state["acc"] = [psum_mx.tile([P, FEAT], F32, name="mx%d" % m) for m in range(LIVE_TILES)]
            if c < FIRST_PART:
                for m, acc in enumerate(state["acc"]):
                    edge_pass(acc, m, c, c == 0, c == FIRST_PART - 1)
                if c == FIRST_PART - 1:
                    for m, acc in enumerate(state["acc"]):
                        nc.scalar.copy(out=first_part[:, m, :], in_=acc[:])
            else:
                missed = (FIRST_PART + CATCH_UP_STEPS - 1) // CATCH_UP_STEPS
                caught_up = range((c - FIRST_PART) * missed, min((c - FIRST_PART + 1) * missed, FIRST_PART))
                for m, acc in enumerate(state["acc"]):
                    for past in caught_up:
                        edge_pass(acc, LIVE_TILES + m, past, past == 0, False)
                    edge_pass(acc, LIVE_TILES + m, c, False, c == PASSES - 1)

        def multiply_late(acc, m, passes):
            for c in passes:
                edge_pass(acc, m, c, c == FIRST_PART, c == PASSES - 1)

        def store_edge_block(m, acc):
            if m < LIVE_TILES:
                block = first_part[:, m, :]
                nc.vector.tensor_tensor(out=block, in0=acc[:], in1=block, op=ALU.add)
            else:
                block = tail.tile([P, FEAT], F32, name="prod", bufs=6)[:]
                nc.vector.tensor_copy(out=block, in_=acc[:])
            nc.sync.dma_start(out=out[2 * FEAT + m * P : 2 * FEAT + (m + 1) * P, :], in_=block)

        last = PASSES - 1

        def one_step(step):
            if step + 2 < PASSES:
                load_gradient(step + 2)
            if 0 <= step + 2 - LAG:
                load_edges(step + 2 - LAG)
            if step == 0:
                build_selectors()
                pick_masks()
                reduce_masks()
            scaled_gradient(step)
            if step == 0:
                build_coefficients()
                nc.scalar.copy(out=node_f32[:], in_=node_bf[:])
            if step >= 3:
                flush_row_sums(step - 3)
                if step - 3 == PASSES_PER_GRAPH - 1:
                    flush_col_sums(0)
            if step >= 1:
                line_of_y(step - 1, SLOT_ORDER if step < last else SLOT_ORDER[VEC_SLOTS:])
            if step >= 2:
                add_line_on_gpsimd(step - 2)
                add_line_on_vector(step - 2, slice(0, VEC_SLOTS))
                transpose_for_col_sums(step - 2)
                transpose_for_row_sums(step - 2)
            if step < last:
                half_shift_on_gpsimd(step)
            if step >= LAG:
                mask_edges(step - LAG)
            if step == last:
                quantise_edges(step - LAG - 1)
                quantise_gradient(step - 3)
                line_of_y_on_vector(step - 1, SLOT_ORDER[:VEC_SLOTS])
                add_line_on_vector(step - 1, slice(VEC_SLOTS, PACK))
                add_line_on_vector(step - 1, slice(0, VEC_SLOTS))
                flush_row_sums(step - 2)
            gradient_dot_y(step)
            if step == 0:
                multiply_masks()
            if LAG + 1 <= step < last:
                quantise_edges(step - LAG - 1)
            line_slope(step)
            if step < last:
                line_shift_on_gpsimd(step)
            if step >= 2:
                regroup_gradient(step - 2)
            if step == last:
                quantise_gradient(step - 2)
            elif step >= 3:
                quantise_gradient(step - 3)
            if step == last:
                line_shift(step)
                regroup_gradient(step - 1)
                line_of_y(step, SLOT_ORDER[VEC_SLOTS:])
                transpose_for_col_sums(step - 1)
                transpose_for_row_sums(step - 1)
                multiply_edges(step - LAG - 1)
                state["late"] = psum_gx.tile([P, FEAT], F32, name="gx")
                multiply_late(state["late"], 0, range(FIRST_PART, step - LAG))
                line_of_y_on_vector(step, SLOT_ORDER[:VEC_SLOTS])
                add_line_on_vector(step, slice(VEC_SLOTS, PACK))
                flush_row_sums(step - 1)
                add_line_on_vector(step, slice(0, VEC_SLOTS))
            elif step >= LAG + 1:
                multiply_edges(step - LAG - 1)
            if step >= LAG:
                regroup_edges(step - LAG, nc.scalar.copy)

        def last_steps():
            transpose_for_row_sums(last)
            transpose_for_col_sums(last)
            regroup_gradient(last)
            mask_edges(last - 1)
            quantise_gradient(last - 1)
            quantise_edges(last - 2)
            flush_row_sums(last)
            row_sums = turn_sums(row_sums_t, psum_rs.tile([P, FEAT], F32, name="rs_ps"))
            late0_ps = state["late"]
            multiply_edges(last - 2)
            flush_col_sums(1)
            regroup_edges(last - 1, nc.vector.tensor_copy)
            node_product(0, 0, row_sums, psum_cs.tile([P, FEAT], F32, name="cs1"))
            node_product(0, 1, row_sums, psum_cs.tile([P, FEAT], F32, name="cs2"))
            mask_edges(last)
            quantise_edges(last - 1)
            col_sums = turn_sums(col_sums_t, psum_cs.tile([P, FEAT], F32, name="cs0"))
            node_product(0, 2, row_sums, psum_cs.tile([P, FEAT], F32, name="cs3"))
            node_product(0, 3, row_sums, psum_cs.tile([P, FEAT], F32, name="cs1"))
            multiply_edges(last - 1)
            late1_ps = psum_rs.tile([P, FEAT], F32, name="rs_ps")
            multiply_late(late1_ps, 1, range(FIRST_PART, last))
            multiply_late(late0_ps, 0, range(last - 2, last))
            regroup_edges(last, nc.vector.tensor_copy)
            quantise_gradient(last)
            quantise_edges(last)
            node_product(FEAT, 0, col_sums, psum_cs.tile([P, FEAT], F32, name="cs2"))
            multiply_edges(last)
            for m, acc in enumerate((late0_ps, late1_ps)):
                multiply_late(acc, m, range(last, PASSES))
            for m, acc in enumerate((*state["acc"], late0_ps, late1_ps)):
                store_edge_block((LIVE_TILES + m) % FBLOCKS, acc)
            for m in range(1, FBLOCKS):
                node_product(FEAT, m, col_sums, psum_cs.tile([P, FEAT], F32, name="cs%d" % (m % 3 + 1)))

        with tc.manual_schedule(
            engines={mybir.EngineType.PE, mybir.EngineType.Activation, mybir.EngineType.DVE, mybir.EngineType.Pool}
        ):
            for step in range(PASSES):
                one_step(step)
            last_steps()
